import numpy as np
import ml_dtypes


def mxq(x, axis, fmt="e4m3"):
    dtype, down = {"e4m3": (ml_dtypes.float8_e4m3fn, 7), "e5m2": (ml_dtypes.float8_e5m2, 14)}[fmt]
    v = np.moveaxis(np.asarray(x, np.float32).astype(ml_dtypes.bfloat16).astype(np.float64), axis, -1)
    blocks = v.reshape(v.shape[:-1] + (-1, 32))
    amax = np.abs(blocks).max(-1, keepdims=True)
    byte = np.maximum(np.where(amax > 0, np.frexp(amax)[1] - 1 + 127, 0) - down, 1)
    scale = np.exp2(byte - 127.0)
    codes = (blocks / scale).astype(np.float32).astype(dtype).astype(np.float64)
    return np.moveaxis((codes * scale).reshape(v.shape), -1, axis)


WIDE = False


def mx_kscale(k):
    if not WIDE:
        return np.ones(k)
    levels = np.array([10, -10, 5, -5, 0])
    a = np.random.permutation(np.resize(levels, k // 512 * 4)).reshape(k // 512, 4)
    idx = np.arange(k)
    return np.exp2(a[idx // 512, idx % 128 // 32])


BF16 = ml_dtypes.bfloat16


def bf(x):
    return np.asarray(x, np.float32).astype(BF16)


def f64(x):
    return np.asarray(x).astype(np.float64)


N, V, M0, M1, M2 = 512, 512, 128, 64, 32
MUL = [(M0, 1), (M1, 3), (M2, 5)]
DX = sum(m * d for m, d in MUL)


def setup_inputs():
    s = mx_kscale(V)
    ws = 8.0 / np.sqrt(V) / s[None, :, None]
    return {"x": bf(np.random.standard_normal((N, DX))),
            "z": bf(np.random.standard_normal((N, V)) * s),
            "w0": bf(np.random.standard_normal((M0, V, M0)) * ws),
            "w1": bf(np.random.standard_normal((M1, V, M1)) * ws),
            "w2": bf(np.random.standard_normal((M2, V, M2)) * ws)}


def reference(x, z, w0, w1, w2):
    x = f64(x)
    zq = mxq(f64(z), 1, "e4m3")
    outs = []
    off = 0
    for (mul, d), w in zip(MUL, (w0, w1, w2)):
        xs = x[:, off:off + mul * d].reshape(-1, mul, d)
        alpha = 1.0 / np.sqrt(mul * V)
        wq = mxq(f64(w), 1, "e4m3")
        t = (zq @ wq.transpose(1, 0, 2).reshape(V, mul * mul)).reshape(-1, mul, mul)
        o = (xs[:, :, None, :] * t[:, :, :, None]).sum(1) * alpha
        outs.append(o.reshape(-1, mul * d))
        off += mul * d
    return np.concatenate(outs, axis=1)

@@ -1,0 +1,278 @@
+from contextlib import ExitStack
+
+import concourse.mybir as mybir
+from concourse.masks import make_identity
+
+F32 = mybir.dt.float32
+BF16 = mybir.dt.bfloat16
+U32 = mybir.dt.uint32
+U8 = mybir.dt.uint8
+FP8X4 = mybir.dt.float8_e4m3fn_x4
+ALU = mybir.AluOpType
+ACT = mybir.ActivationFunctionType
+
+P = 128
+N = 512
+V = 512
+TILES = N // P
+DX = 480
+CHUNK = 4096
+BANK = 512
+
+FLOPS = 2 * N * V * (128 * 128 + 64 * 64 + 32 * 32) + 2 * N * (128 * 128 + 64 * 64 * 3 + 32 * 32 * 5)
+
+PIN = True
+
+
+def tile_selfconnectionintro_kernel(tc, x, z, w0, w1, w2, out):
+    nc = tc.nc
+    with ExitStack() as ctx:
+        const = ctx.enter_context(tc.tile_pool(name="const", bufs=1))
+        raw0_pool = ctx.enter_context(tc.tile_pool(name="raw0", bufs=4))
+        grp0_pool = ctx.enter_context(tc.tile_pool(name="grp0", bufs=2))
+        cod0_pool = ctx.enter_context(tc.tile_pool(name="cod0", bufs=2))
+        grpa_pool = ctx.enter_context(tc.tile_pool(name="grpa", bufs=2))
+        prod_pool = ctx.enter_context(tc.tile_pool(name="prod", bufs=8))
+        ps_acc = ctx.enter_context(tc.psum_pool(name="psacc", bufs=1))
+        ps_b0 = ctx.enter_context(tc.psum_pool(name="psb0", bufs=4))
+        ps_ba = ctx.enter_context(tc.psum_pool(name="psba", bufs=3))
+        if PIN:
+            ctx.enter_context(tc.manual_schedule())
+
+        ident = const.tile([P, P], F32, name="ident")
+        z_sb = const.tile([P, TILES * V], BF16, name="z_sb")
+        x_sb = const.tile([P, TILES, DX], BF16, name="x_sb")
+        xs = const.tile([P, TILES, DX], F32, name="xs")
+        zg = const.tile([P, 4 * N], BF16, name="zg", align_bytes=64)
+        zq = const.tile([P, N], U32, name="zq", align_bytes=64)
+        zs = const.tile([P, N], U8, name="zs", align_bytes=64)
+        acc1 = const.tile([P, TILES, 2, 3, 64], F32, name="acc1")
+        acc2 = const.tile([P, TILES, 2, 5, 32], F32, name="acc2")
+        fin = const.tile([P, TILES, DX], F32, name="fin")
+        ot_sb = const.tile([P, N], F32, name="ot_sb")
+        o_t = ps_acc.tile([P, N], F32, name="o_t")
+
+        a_chunks = [(w2, 0, 32, 32, 5, 320, acc2)]
+        for a in range(4):
+            a_chunks.append((w1, 16 * a, 16, 64, 3, 128, acc1))
+        raw_a = []
+        cod_a = []
+        sca_a = []
+        for a in range(5):
+            uch = a_chunks[a][2]
+            mul = a_chunks[a][3]
+            raw_a.append(const.tile([P, uch, 4 * mul], BF16, name="raw_a%d" % a))
+            cod_a.append(const.tile([P, CHUNK // 4], U32, name="cod_a%d" % a, align_bytes=64))
+            sca_a.append(const.tile([P, CHUNK // 4], U8, name="sca_a%d" % a, align_bytes=64))
+
+        def load_a(a):
+            w, u0, uch = a_chunks[a][0], a_chunks[a][1], a_chunks[a][2]
+            nc.sync.dma_start(
+                out=raw_a[a][:], in_=w[u0 : u0 + uch].rearrange("u (p j) c -> p u (j c)", j=4)
+            )
+
+        raw0 = {}
+        grp0 = {}
+        cod0 = {}
+        sca0 = {}
+        grpa = {}
+
+        def load_0(k):
+            raw0[k] = raw0_pool.tile([P, 8, 512], BF16, name="raw0t")
+            nc.sync.dma_start(
+                out=raw0[k][:], in_=w0[8 * k : 8 * k + 8].rearrange("u (p j) c -> p u (j c)", j=4)
+            )
+
+        def regroup(eng, raw, grp, mul, lo, hi):
+            if eng == "s":
+                for u in range(lo, hi):
+                    nc.scalar.copy(
+                        out=grp[:, u * 4 * mul : (u + 1) * 4 * mul].rearrange(
+                            "p (c i t) -> p c t i", i=4, t=4
+                        ),
+                        in_=raw[:, u, :].rearrange("p (t c i) -> p c t i", t=4, i=4),
+                    )
+                return
+            dst = grp[:, lo * 4 * mul : hi * 4 * mul].rearrange("p (u c j) -> p u c j", c=mul, j=4)
+            src = raw[:, lo:hi, :].rearrange("p u (j c) -> p u c j", j=4)
+            if eng == "v":
+                nc.vector.tensor_copy(out=dst, in_=src)
+            else:
+                nc.gpsimd.tensor_scalar(
+                    out=dst, in0=src, scalar1=1.0, scalar2=0.0, op0=ALU.mult, op1=ALU.add
+                )
+
+        def quantise(grp, cod, sca):
+            nc.vector.quantize_mx(out=cod[:].bitcast(FP8X4), scales=sca[:], in_=grp[:])
+
+        def mx_pass(bank, i, cod, sca, h):
+            nc.tensor.matmul_mx(
+                out=bank[:],
+                lhsT=zq[:, P * i : P * (i + 1)].bitcast(FP8X4),
+                lhsT_scale=zs[:, P * i : P * (i + 1)],
+                rhs=cod[:, BANK * h : BANK * (h + 1)].bitcast(FP8X4),
+                rhs_scale=sca[:, BANK * h : BANK * (h + 1)],
+                start=True,
+                stop=True,
+            )
+
+        nc.sync.dma_start(out=z_sb[:].rearrange("g (i v) -> g i v", i=TILES), in_=z.rearrange("(i g) v -> g i v", g=P))
+        nc.sync.dma_start(out=x_sb[:], in_=x.rearrange("(i g) c -> g i c", g=P))
+        load_a(0)
+        load_0(0)
+        load_0(1)
+        load_a(1)
+        load_0(2)
+        load_0(3)
+        load_a(2)
+        load_a(3)
+        load_a(4)
+
+        make_identity(nc, ident[:])
+        nc.vector.memset(acc1[:], 0.0)
+        nc.vector.memset(acc2[:], 0.0)
+
+        zw = z_sb[:].bitcast(F32).rearrange("g (i p u) -> g i u p", i=TILES, u=2)
+        zgf = zg[:].bitcast(F32).rearrange("p (b i g u) -> p b i g u", b=2, i=2, u=2)
+        for b in range(2):
+            zt = ps_ba.tile([P, 2, 2, P], F32, name="bank_a")
+            for ii in range(2):
+                for u in range(2):
+                    nc.tensor.transpose(out=zt[:, ii, u, :], in_=zw[:, 2 * b + ii, u, :], identity=ident[:])
+            nc.vector.tensor_copy(out=zgf[:, b], in_=zt[:].rearrange("p i u g -> p i g u"))
+
+        nc.scalar.activation(out=xs[:, :, 0:128], in_=x_sb[:, :, 0:128], func=ACT.Copy, scale=1.0 / 256.0)
+        nc.scalar.activation(
+            out=xs[:, :, 128:320], in_=x_sb[:, :, 128:320], func=ACT.Copy, scale=1.0 / (64.0 * 512.0) ** 0.5
+        )
+        nc.scalar.activation(out=xs[:, :, 320:480], in_=x_sb[:, :, 320:480], func=ACT.Copy, scale=1.0 / 128.0)
+
+        grpa[0] = grpa_pool.tile([P, CHUNK], BF16, name="grpat", align_bytes=64)
+        regroup("v", raw_a[0], grpa[0], 32, 0, 16)
+        regroup("s", raw_a[0], grpa[0], 32, 16, 24)
+        regroup("g", raw_a[0], grpa[0], 32, 24, 32)
+        quantise(zg, zq, zs)
+        for k in range(2):
+            grp0[k] = grp0_pool.tile([P, CHUNK], BF16, name="grp0t", align_bytes=64)
+            regroup("v", raw0[k], grp0[k], 128, 0, 4)
+            regroup("s", raw0[k], grp0[k], 128, 4, 6)
+            regroup("g", raw0[k], grp0[k], 128, 6, 8)
+            if k == 0:
+                quantise(grpa[0], cod_a[0], sca_a[0])
+        cod0[0] = cod0_pool.tile([P, CHUNK // 4], U32, name="cod0t", align_bytes=64)
+        sca0[0] = cod0_pool.tile([P, CHUNK // 4], U8, name="sca0t", align_bytes=64)
+        quantise(grp0[0], cod0[0], sca0[0])
+
+        a_banks = [(a, h, i) for a in range(5) for h in range(2) for i in range(TILES)]
+        bank_a = {}
+
+        def a_pass(j):
+            a, h, i = a_banks[j]
+            bank_a[j] = ps_ba.tile([P, BANK], F32, name="bank_a")
+            mx_pass(bank_a[j], i, cod_a[a], sca_a[a], h)
+
+        units = []
+        for j in range(len(a_banks)):
+            for part in range(a_chunks[a_banks[j][0]][2] // 16):
+                units.append((j, part))
+
+        def do_unit(n):
+            j, part = units[n]
+            a, h, i = a_banks[j]
+            u0, uch, mul, d, off, acc = a_chunks[a][1:]
+            if part == 0 and j + 1 < len(a_banks):
+                a_pass(j + 1)
+            for uu in range(8 * part, 8 * part + 8):
+                u = u0 + h * (uch // 2) + uu
+                for m in range(d):
+                    col = off + u * d + m
+                    nc.vector.scalar_tensor_tensor(
+                        out=acc[:, i, uu % 2, m, :],
+                        in0=bank_a[j][:, uu * mul : (uu + 1) * mul],
+                        scalar=xs[:, i, col : col + 1],
+                        in1=acc[:, i, uu % 2, m, :],
+                        op0=ALU.mult,
+                        op1=ALU.add,
+                    )
+
+        a_pass(0)
+
+        prod = {}
+        STEPS = 32
+
+        def transposes(t):
+            for i in range(TILES):
+                for q in range(4):
+                    nc.tensor.matmul(
+                        out=o_t[:, P * i : P * (i + 1)],
+                        lhsT=prod[(t, i)][:, P * q : P * (q + 1)],
+                        rhs=ident[:],
+                        is_transpose=True,
+                        start=(t == 0 and i == 0 and q == 0),
+                        stop=(t == STEPS - 1 and i == TILES - 1 and q == 3),
+                    )
+
+        next_unit = 0
+        for t in range(STEPS):
+            k, h = t // 2, t % 2
+            if h == 0 and k + 4 < 16:
+                load_0(k + 4)
+            if k + 2 < 16:
+                if h == 0:
+                    grp0[k + 2] = grp0_pool.tile([P, CHUNK], BF16, name="grp0t", align_bytes=64)
+                regroup("g", raw0[k + 2], grp0[k + 2], 128, 3 * h, 3 * h + 3)
+                regroup("s", raw0[k + 2], grp0[k + 2], 128, 6 + h, 7 + h)
+            a, r = (k + 2) // 3, (k + 2) % 3
+            if 1 <= a <= 4 and r < 2:
+                if r == 0 and h == 0:
+                    grpa[a] = grpa_pool.tile([P, CHUNK], BF16, name="grpat", align_bytes=64)
+                piece = 2 * r + h
+                regroup("g", raw_a[a], grpa[a], 64, 4 * piece, 4 * piece + 4)
+            if h == 0 and k % 3 == 0 and 1 <= k // 3 <= 4:
+                quantise(grpa[k // 3], cod_a[k // 3], sca_a[k // 3])
+            if h == 1 and k + 1 < 16:
+                cod0[k + 1] = cod0_pool.tile([P, CHUNK // 4], U32, name="cod0t", align_bytes=64)
+                sca0[k + 1] = cod0_pool.tile([P, CHUNK // 4], U8, name="sca0t", align_bytes=64)
+                quantise(grp0[k + 1], cod0[k + 1], sca0[k + 1])
+            banks = []
+            for i in range(TILES):
+                bank = ps_b0.tile([P, BANK], F32, name="bank_0")
+                mx_pass(bank, i, cod0[k], sca0[k], h)
+                banks.append(bank)
+            for i in range(TILES):
+                prod[(t, i)] = prod_pool.tile([P, BANK], F32, name="prodt")
+                for q in range(4):
+                    u = 8 * k + 4 * h + q
+                    nc.scalar.activation(
+                        out=prod[(t, i)][:, P * q : P * (q + 1)],
+                        in_=banks[i][:, P * q : P * (q + 1)],
+                        func=ACT.Copy,
+                        scale=xs[:, i, u : u + 1],
+                    )
+            for n in range(2 - h):
+                do_unit(next_unit)
+                next_unit += 1
+            if t > 0:
+                transposes(t - 1)
+        transposes(STEPS - 1)
+
+        out_v = out.rearrange("(i g) c -> g i c", g=P)
+        nc.vector.tensor_tensor(
+            out=fin[:, :, 128:320].rearrange("p i (c m) -> p i c m", m=3),
+            in0=acc1[:, :, 0].rearrange("p i m c -> p i c m"),
+            in1=acc1[:, :, 1].rearrange("p i m c -> p i c m"),
+            op=ALU.add,
+        )
+        nc.vector.tensor_tensor(
+            out=fin[:, :, 320:480].rearrange("p i (c m) -> p i c m", m=5),
+            in0=acc2[:, :, 0].rearrange("p i m c -> p i c m"),
+            in1=acc2[:, :, 1].rearrange("p i m c -> p i c m"),
+            op=ALU.add,
+        )
+        nc.sync.dma_start(out=out_v[:, :, 128:480], in_=fin[:, :, 128:480])
+        nc.scalar.copy(out=ot_sb[:], in_=o_t[:])
+        back = ps_b0.tile([P, BANK], F32, name="bank_0")
+        for i in range(TILES):
+            nc.tensor.transpose(out=back[:, P * i : P * (i + 1)], in_=ot_sb[:, P * i : P * (i + 1)], identity=ident[:])
+        nc.scalar.copy(out=fin[:, :, 0:128], in_=back[:].rearrange("p (i c) -> p i c", i=TILES))
+        nc.sync.dma_start(out=out_v[:, :, 0:128], in_=fin[:, :, 0:128])

@@ -21,7 +21,7 @@ BANK = 512
 
 FLOPS = 2 * N * V * (128 * 128 + 64 * 64 + 32 * 32) + 2 * N * (128 * 128 + 64 * 64 * 3 + 32 * 32 * 5)
 
-PIN = True
+PIN = False
 
 
 def tile_selfconnectionintro_kernel(tc, x, z, w0, w1, w2, out):

@@ -16,28 +16,35 @@ N = 512
 V = 512
 TILES = N // P
 DX = 480
-CHUNK = 4096
 BANK = 512
+HALF = 2048
 
 FLOPS = 2 * N * V * (128 * 128 + 64 * 64 + 32 * 32) + 2 * N * (128 * 128 + 64 * 64 * 3 + 32 * 32 * 5)
 
-PIN = False
+STEPS = 32
+SPLIT_A = (96, 32, 0)
+SPLIT_B = (0, 48, 16)
+SPLIT_P = (0, 88, 40)
+SPLIT_P2 = (0, 20, 12)
+B_OFF = 3
+B_NUM, B_DEN = 3, 2
+LAG = 1
+U_NUM, U_DEN = 3, 1
 
 
 def tile_selfconnectionintro_kernel(tc, x, z, w0, w1, w2, out):
     nc = tc.nc
     with ExitStack() as ctx:
         const = ctx.enter_context(tc.tile_pool(name="const", bufs=1))
-        raw0_pool = ctx.enter_context(tc.tile_pool(name="raw0", bufs=4))
-        grp0_pool = ctx.enter_context(tc.tile_pool(name="grp0", bufs=2))
-        cod0_pool = ctx.enter_context(tc.tile_pool(name="cod0", bufs=2))
+        raw_pool = ctx.enter_context(tc.tile_pool(name="raw", bufs=5))
         grpa_pool = ctx.enter_context(tc.tile_pool(name="grpa", bufs=2))
-        prod_pool = ctx.enter_context(tc.tile_pool(name="prod", bufs=8))
+        grpb_pool = ctx.enter_context(tc.tile_pool(name="grpb", bufs=2))
+        coda_pool = ctx.enter_context(tc.tile_pool(name="coda", bufs=4))
+        prod_pool = ctx.enter_context(tc.tile_pool(name="prod", bufs=6))
         ps_acc = ctx.enter_context(tc.psum_pool(name="psacc", bufs=1))
-        ps_b0 = ctx.enter_context(tc.psum_pool(name="psb0", bufs=4))
-        ps_ba = ctx.enter_context(tc.psum_pool(name="psba", bufs=3))
-        if PIN:
-            ctx.enter_context(tc.manual_schedule())
+        ps_a = ctx.enter_context(tc.psum_pool(name="psa", bufs=4))
+        ps_b = ctx.enter_context(tc.psum_pool(name="psb", bufs=2))
+        ctx.enter_context(tc.manual_schedule())
 
         ident = const.tile([P, P], F32, name="ident")
         z_sb = const.tile([P, TILES * V], BF16, name="z_sb")
@@ -46,233 +53,322 @@ def tile_selfconnectionintro_kernel(tc, x, z, w0, w1, w2, out):
         zg = const.tile([P, 4 * N], BF16, name="zg", align_bytes=64)
         zq = const.tile([P, N], U32, name="zq", align_bytes=64)
         zs = const.tile([P, N], U8, name="zs", align_bytes=64)
-        acc1 = const.tile([P, TILES, 2, 3, 64], F32, name="acc1")
-        acc2 = const.tile([P, TILES, 2, 5, 32], F32, name="acc2")
         fin = const.tile([P, TILES, DX], F32, name="fin")
-        ot_sb = const.tile([P, N], F32, name="ot_sb")
-        o_t = ps_acc.tile([P, N], F32, name="o_t")
-
-        a_chunks = [(w2, 0, 32, 32, 5, 320, acc2)]
+        raw_b = [const.tile([P, 32, 128], BF16, name="raw_b0")]
         for a in range(4):
-            a_chunks.append((w1, 16 * a, 16, 64, 3, 128, acc1))
-        raw_a = []
-        cod_a = []
-        sca_a = []
-        for a in range(5):
-            uch = a_chunks[a][2]
-            mul = a_chunks[a][3]
-            raw_a.append(const.tile([P, uch, 4 * mul], BF16, name="raw_a%d" % a))
-            cod_a.append(const.tile([P, CHUNK // 4], U32, name="cod_a%d" % a, align_bytes=64))
-            sca_a.append(const.tile([P, CHUNK // 4], U8, name="sca_a%d" % a, align_bytes=64))
+            raw_b.append(const.tile([P, 16, 256], BF16, name="raw_b%d" % (a + 1)))
+        cod_b = [const.tile([P, 1024], U32, name="cod_b%d" % a, align_bytes=64) for a in range(5)]
+        sca_b = [const.tile([P, 1024], U8, name="sca_b%d" % a, align_bytes=64) for a in range(5)]
 
-        def load_a(a):
-            w, u0, uch = a_chunks[a][0], a_chunks[a][1], a_chunks[a][2]
-            nc.sync.dma_start(
-                out=raw_a[a][:], in_=w[u0 : u0 + uch].rearrange("u (p j) c -> p u (j c)", j=4)
-            )
-
-        raw0 = {}
-        grp0 = {}
-        cod0 = {}
-        sca0 = {}
-        grpa = {}
-
-        def load_0(k):
-            raw0[k] = raw0_pool.tile([P, 8, 512], BF16, name="raw0t")
-            nc.sync.dma_start(
-                out=raw0[k][:], in_=w0[8 * k : 8 * k + 8].rearrange("u (p j) c -> p u (j c)", j=4)
-            )
-
-        def regroup(eng, raw, grp, mul, lo, hi):
-            if eng == "s":
-                for u in range(lo, hi):
-                    nc.scalar.copy(
-                        out=grp[:, u * 4 * mul : (u + 1) * 4 * mul].rearrange(
-                            "p (c i t) -> p c t i", i=4, t=4
-                        ),
-                        in_=raw[:, u, :].rearrange("p (t c i) -> p c t i", t=4, i=4),
-                    )
+        def regroup(eng, raw, grp, mul, c0, c1):
+            if c1 <= c0:
                 return
-            dst = grp[:, lo * 4 * mul : hi * 4 * mul].rearrange("p (u c j) -> p u c j", c=mul, j=4)
-            src = raw[:, lo:hi, :].rearrange("p u (j c) -> p u c j", j=4)
+            dst = grp.rearrange("p (u c j) -> p u c j", c=mul, j=4)[:, :, c0:c1, :]
+            src = raw.rearrange("p u (j c) -> p u c j", j=4)[:, :, c0:c1, :]
             if eng == "v":
-                nc.vector.tensor_copy(out=dst, in_=src)
-            else:
-                nc.gpsimd.tensor_scalar(
-                    out=dst, in0=src, scalar1=1.0, scalar2=0.0, op0=ALU.mult, op1=ALU.add
+                nc.vector.tensor_copy(
+                    out=grp.rearrange("p (u c i j) -> p u c j i", c=mul // 4, i=4, j=4)[:, :, c0 // 4 : c1 // 4, :, :],
+                    in_=raw.rearrange("p u (j c i) -> p u c j i", j=4, i=4)[:, :, c0 // 4 : c1 // 4, :, :],
                 )
+            elif eng == "s":
+                nc.scalar.copy(out=dst, in_=src)
+            else:
+                nc.gpsimd.tensor_scalar(out=dst, in0=src, scalar1=1.0, scalar2=0.0, op0=ALU.mult, op1=ALU.add)
+
+        def regroup3(raw, grp, mul, split, order):
+            g, v, s = split
+            for e in order:
+                if e == "g":
+                    regroup("g", raw, grp, mul, 0, g)
+                elif e == "v":
+                    regroup("v", raw, grp, mul, g, g + v)
+                else:
+                    regroup("s", raw, grp, mul, g + v, g + v + s)
 
         def quantise(grp, cod, sca):
-            nc.vector.quantize_mx(out=cod[:].bitcast(FP8X4), scales=sca[:], in_=grp[:])
+            nc.vector.quantize_mx(out=cod.bitcast(FP8X4), scales=sca, in_=grp)
 
-        def mx_pass(bank, i, cod, sca, h):
+        def mx_pass(bank, i, cod, sca):
             nc.tensor.matmul_mx(
                 out=bank[:],
                 lhsT=zq[:, P * i : P * (i + 1)].bitcast(FP8X4),
                 lhsT_scale=zs[:, P * i : P * (i + 1)],
-                rhs=cod[:, BANK * h : BANK * (h + 1)].bitcast(FP8X4),
-                rhs_scale=sca[:, BANK * h : BANK * (h + 1)],
+                rhs=cod.bitcast(FP8X4),
+                rhs_scale=sca,
                 start=True,
                 stop=True,
             )
 
+        raw_a = {}
+        grp_a = {}
+        cod_a = {}
+        sca_a = {}
+
+        def load_a(k, halves=False):
+            raw_a[k] = raw_pool.tile([P, 8, 512], BF16, name="rawt")
+            for lo, hi in ((0, 4), (4, 8)) if halves else ((0, 8),):
+                nc.sync.dma_start(
+                    out=raw_a[k][:, lo:hi, :], in_=w0[8 * k + lo : 8 * k + hi].rearrange("u (p j) c -> p u (j c)", j=4)
+                )
+
+        def load_b(a, lo=0, hi=None):
+            w = w2 if a == 0 else w1[16 * (a - 1) : 16 * a]
+            hi = hi or (32 if a == 0 else 16)
+            nc.sync.dma_start(out=raw_b[a][:, lo:hi, :], in_=w[lo:hi].rearrange("u (p j) c -> p u (j c)", j=4))
+
+        def regroup_a(s, split, order):
+            if s not in grp_a:
+                grp_a[s] = grpa_pool.tile([P, HALF], BF16, name="grpat", align_bytes=64)
+            regroup3(raw_a[s // 2][:, 4 * (s % 2) : 4 * (s % 2) + 4, :], grp_a[s][:], 128, split, order)
+
+        def quantise_a(s):
+            cod_a[s] = coda_pool.tile([P, BANK], U32, name="codat", align_bytes=64)
+            sca_a[s] = coda_pool.tile([P, BANK], U8, name="scaat", align_bytes=64)
+            quantise(grp_a[s][:], cod_a[s][:], sca_a[s][:])
+
+        grp_b = {}
+
+        def regroup_b(m, split, order):
+            if m not in grp_b:
+                grp_b[m] = grpb_pool.tile([P, 1024], BF16, name="grpbt", align_bytes=64)
+            regroup3(raw_b[1 + m // 4][:, 4 * (m % 4) : 4 * (m % 4) + 4, :], grp_b[m][:], 64, split, order)
+
+        def quantise_b(m):
+            a, r = 1 + m // 4, m % 4
+            quantise(grp_b[m][:], cod_b[a][:, 256 * r : 256 * (r + 1)], sca_b[a][:, 256 * r : 256 * (r + 1)])
+
         nc.sync.dma_start(out=z_sb[:].rearrange("g (i v) -> g i v", i=TILES), in_=z.rearrange("(i g) v -> g i v", g=P))
+        load_b(0, 0, 16)
         nc.sync.dma_start(out=x_sb[:], in_=x.rearrange("(i g) c -> g i c", g=P))
-        load_a(0)
-        load_0(0)
-        load_0(1)
-        load_a(1)
-        load_0(2)
-        load_0(3)
+        load_a(0, True)
+        load_a(1, True)
         load_a(2)
-        load_a(3)
-        load_a(4)
+        load_b(0, 16, 32)
 
         make_identity(nc, ident[:])
-        nc.vector.memset(acc1[:], 0.0)
-        nc.vector.memset(acc2[:], 0.0)
+        nc.vector.memset(fin[:, :, 0:128], 0.0)
+        perm = []
+        fold = []
+        for mul in (32, 64):
+            pm = const.tile([P, P], F32, name="perm%d" % mul)
+            nc.gpsimd.tensor_scalar(
+                out=pm[:].rearrange("p (c m) -> p c m", c=mul),
+                in0=ident[:].rearrange("p (m c) -> p c m", c=mul),
+                scalar1=1.0,
+                scalar2=0.0,
+                op0=ALU.mult,
+                op1=ALU.add,
+            )
+            perm.append(pm)
+            sm = const.tile([P, mul], F32, name="fold%d" % mul)
+            nc.vector.tensor_reduce(out=sm[:], in_=ident[:].rearrange("p (q c) -> p c q", c=mul), axis=mybir.AxisListType.X, op=ALU.add)
+            fold.append(sm)
 
         zw = z_sb[:].bitcast(F32).rearrange("g (i p u) -> g i u p", i=TILES, u=2)
         zgf = zg[:].bitcast(F32).rearrange("p (b i g u) -> p b i g u", b=2, i=2, u=2)
+        zts = []
         for b in range(2):
-            zt = ps_ba.tile([P, 2, 2, P], F32, name="bank_a")
+            zt = ps_a.tile([P, 2, 2, P], F32, name="bank_a")
             for ii in range(2):
                 for u in range(2):
                     nc.tensor.transpose(out=zt[:, ii, u, :], in_=zw[:, 2 * b + ii, u, :], identity=ident[:])
-            nc.vector.tensor_copy(out=zgf[:, b], in_=zt[:].rearrange("p i u g -> p i g u"))
-
-        nc.scalar.activation(out=xs[:, :, 0:128], in_=x_sb[:, :, 0:128], func=ACT.Copy, scale=1.0 / 256.0)
-        nc.scalar.activation(
-            out=xs[:, :, 128:320], in_=x_sb[:, :, 128:320], func=ACT.Copy, scale=1.0 / (64.0 * 512.0) ** 0.5
-        )
+            zts.append(zt)
+        grp2 = {}
+        grp2[0] = grpb_pool.tile([P, HALF], BF16, name="grp2t", align_bytes=64)
+        regroup3(raw_b[0][:, 0:16, :], grp2[0][:], 32, SPLIT_P2, "vs")
+        nc.vector.tensor_copy(out=zgf[:, 0], in_=zts[0][:].rearrange("p i u g -> p i g u"))
+        nc.vector.quantize_mx(out=cod_b[0][:, 0:BANK].bitcast(FP8X4), scales=sca_b[0][:, 0:BANK], in_=grp2[0][:])
         nc.scalar.activation(out=xs[:, :, 320:480], in_=x_sb[:, :, 320:480], func=ACT.Copy, scale=1.0 / 128.0)
+        nc.scalar.copy(out=zgf[:, 1], in_=zts[1][:].rearrange("p i u g -> p i g u"))
+        nc.gpsimd.tensor_scalar(out=xs[:, :, 0:128], in0=x_sb[:, :, 0:128], scalar1=1.0 / 256.0, scalar2=0.0, op0=ALU.mult, op1=ALU.add)
+        regroup_a(0, SPLIT_P, "vs")
+        quantise(zg[:], zq[:], zs[:])
+        quantise_a(0)
+        nc.gpsimd.tensor_scalar(
+            out=xs[:, :, 128:320], in0=x_sb[:, :, 128:320], scalar1=1.0 / (64.0 * 512.0) ** 0.5, scalar2=0.0, op0=ALU.mult, op1=ALU.add
+        )
 
-        grpa[0] = grpa_pool.tile([P, CHUNK], BF16, name="grpat", align_bytes=64)
-        regroup("v", raw_a[0], grpa[0], 32, 0, 16)
-        regroup("s", raw_a[0], grpa[0], 32, 16, 24)
-        regroup("g", raw_a[0], grpa[0], 32, 24, 32)
-        quantise(zg, zq, zs)
-        for k in range(2):
-            grp0[k] = grp0_pool.tile([P, CHUNK], BF16, name="grp0t", align_bytes=64)
-            regroup("v", raw0[k], grp0[k], 128, 0, 4)
-            regroup("s", raw0[k], grp0[k], 128, 4, 6)
-            regroup("g", raw0[k], grp0[k], 128, 6, 8)
-            if k == 0:
-                quantise(grpa[0], cod_a[0], sca_a[0])
-        cod0[0] = cod0_pool.tile([P, CHUNK // 4], U32, name="cod0t", align_bytes=64)
-        sca0[0] = cod0_pool.tile([P, CHUNK // 4], U8, name="sca0t", align_bytes=64)
-        quantise(grp0[0], cod0[0], sca0[0])
+        b_banks = [(a, h, i) for a in range(5) for h in range(2) for i in range(TILES)]
+        units = []
+        for n in range(len(b_banks)):
+            for part in range(4 if b_banks[n][0] == 0 else 2):
+                units.append((n, part))
+        bank_b = {}
+        prod = {}
+        acc_t = {}
 
-        a_banks = [(a, h, i) for a in range(5) for h in range(2) for i in range(TILES)]
+        def b_pass(n):
+            a, h, i = b_banks[n]
+            bank_b[n] = ps_b.tile([P, BANK], F32, name="bank_b")
+            mx_pass(bank_b[n], i, cod_b[a][:, BANK * h : BANK * (h + 1)], sca_b[a][:, BANK * h : BANK * (h + 1)])
+
+        def unit_products(j):
+            n, part = units[j]
+            a, h, i = b_banks[n]
+            prod[j] = prod_pool.tile([P, 768], F32, name="prodt")
+            for q in range(4):
+                ul = 4 * part + q
+                if a == 0:
+                    u = 16 * h + ul
+                    for m in range(5):
+                        slot = 4 * q + m if m < 4 else 16 + q
+                        nc.scalar.activation(
+                            out=prod[j][:, 32 * slot : 32 * slot + 32],
+                            in_=bank_b[n][:, 32 * ul : 32 * ul + 32],
+                            func=ACT.Copy,
+                            scale=xs[:, i, 320 + 5 * u + m : 320 + 5 * u + m + 1],
+                        )
+                else:
+                    u = 16 * (a - 1) + 8 * h + ul
+                    for m in range(3):
+                        slot = 6 * (q // 2) + (2 * (q % 2) + m if m < 2 else 4 + q % 2)
+                        nc.scalar.activation(
+                            out=prod[j][:, 64 * slot : 64 * slot + 64],
+                            in_=bank_b[n][:, 64 * ul : 64 * ul + 64],
+                            func=ACT.Copy,
+                            scale=xs[:, i, 128 + 3 * u + m : 128 + 3 * u + m + 1],
+                        )
+
+        first_sum = {}
+
+        def unit_sums(j):
+            n, part = units[j]
+            a, h, i = b_banks[n]
+            blk = 0 if a == 0 else 1
+            if blk not in acc_t:
+                acc_t[blk] = (ps_acc.tile([P, N], F32, name="acc_x"), ps_acc.tile([P, N], F32, name="acc_y"))
+            last_unit = 31 if a == 0 else 95
+            kinds = [0, 0, 0, 0, 1] if a == 0 else [0, 0, 1, 0, 0, 1]
+            for b in range(len(kinds)):
+                kd = kinds[b]
+                nc.tensor.matmul(
+                    out=acc_t[blk][kd][:, P * i : P * (i + 1)],
+                    lhsT=prod[j][:, P * b : P * (b + 1)],
+                    rhs=ident[:],
+                    is_transpose=True,
+                    start=((blk, kd) not in first_sum),
+                    stop=(j == last_unit and b == (len(kinds) - 1 if kd == 1 else len(kinds) - 2)),
+                )
+                first_sum[(blk, kd)] = True
+
+        t_sb = {}
+
+        def evacuate(blk, engines):
+            for kd in range(2):
+                t_sb[(blk, kd)] = const.tile([P, N], F32, name="t_sb%d%d" % (blk, kd))
+                if engines[kd] == "s":
+                    nc.scalar.copy(out=t_sb[(blk, kd)][:], in_=acc_t[blk][kd][:])
+                else:
+                    nc.vector.tensor_copy(out=t_sb[(blk, kd)][:], in_=acc_t[blk][kd][:])
+
+        def finish(blk, pool, tag, copier):
+            mul, d, off = (32, 5, 320) if blk == 0 else (64, 3, 128)
+            full = P // mul
+            for b in range(2):
+                b_ps = pool.tile([P, 2, mul, d], F32, name=tag)
+                for ii in range(2):
+                    i = 2 * b + ii
+                    nc.tensor.matmul(
+                        out=b_ps[:, ii, :, 0:full],
+                        lhsT=t_sb[(blk, 0)][:, P * i : P * (i + 1)],
+                        rhs=perm[blk][:],
+                        start=True,
+                        stop=True,
+                    )
+                    nc.tensor.matmul(
+                        out=b_ps[:, ii, :, full],
+                        lhsT=t_sb[(blk, 1)][:, P * i : P * (i + 1)],
+                        rhs=fold[blk][:],
+                        start=True,
+                        stop=True,
+                    )
+                if copier[b] == "s":
+                    nc.scalar.copy(
+                        out=fin[:, 2 * b : 2 * b + 2, off : off + mul * d], in_=b_ps[:].rearrange("p i c m -> p i (c m)")
+                    )
+                else:
+                    nc.vector.tensor_copy(
+                        out=fin[:, 2 * b : 2 * b + 2, off : off + mul * d], in_=b_ps[:].rearrange("p i c m -> p i (c m)")
+                    )
+
+        b_pass(0)
+        b_pass(1)
+        next_bank = 2
+        regroup_a(1, SPLIT_P, "vs")
+
+        def unit_lo(t):
+            return min(96, (U_NUM * t) // U_DEN)
+
+        b_step = {}
+        for m in range(16):
+            b_step[B_OFF + (B_NUM * m) // B_DEN] = m
+        out_v = out.rearrange("(i g) c -> g i c", g=P)
         bank_a = {}
 
-        def a_pass(j):
-            a, h, i = a_banks[j]
-            bank_a[j] = ps_ba.tile([P, BANK], F32, name="bank_a")
-            mx_pass(bank_a[j], i, cod_a[a], sca_a[a], h)
-
-        units = []
-        for j in range(len(a_banks)):
-            for part in range(a_chunks[a_banks[j][0]][2] // 16):
-                units.append((j, part))
-
-        def do_unit(n):
-            j, part = units[n]
-            a, h, i = a_banks[j]
-            u0, uch, mul, d, off, acc = a_chunks[a][1:]
-            if part == 0 and j + 1 < len(a_banks):
-                a_pass(j + 1)
-            for uu in range(8 * part, 8 * part + 8):
-                u = u0 + h * (uch // 2) + uu
-                for m in range(d):
-                    col = off + u * d + m
-                    nc.vector.scalar_tensor_tensor(
-                        out=acc[:, i, uu % 2, m, :],
-                        in0=bank_a[j][:, uu * mul : (uu + 1) * mul],
-                        scalar=xs[:, i, col : col + 1],
-                        in1=acc[:, i, uu % 2, m, :],
-                        op0=ALU.mult,
-                        op1=ALU.add,
-                    )
-
-        a_pass(0)
-
-        prod = {}
-        STEPS = 32
-
-        def transposes(t):
-            for i in range(TILES):
-                for q in range(4):
-                    nc.tensor.matmul(
-                        out=o_t[:, P * i : P * (i + 1)],
-                        lhsT=prod[(t, i)][:, P * q : P * (q + 1)],
-                        rhs=ident[:],
-                        is_transpose=True,
-                        start=(t == 0 and i == 0 and q == 0),
-                        stop=(t == STEPS - 1 and i == TILES - 1 and q == 3),
-                    )
-
-        next_unit = 0
         for t in range(STEPS):
-            k, h = t // 2, t % 2
-            if h == 0 and k + 4 < 16:
-                load_0(k + 4)
-            if k + 2 < 16:
-                if h == 0:
-                    grp0[k + 2] = grp0_pool.tile([P, CHUNK], BF16, name="grp0t", align_bytes=64)
-                regroup("g", raw0[k + 2], grp0[k + 2], 128, 3 * h, 3 * h + 3)
-                regroup("s", raw0[k + 2], grp0[k + 2], 128, 6 + h, 7 + h)
-            a, r = (k + 2) // 3, (k + 2) % 3
-            if 1 <= a <= 4 and r < 2:
-                if r == 0 and h == 0:
-                    grpa[a] = grpa_pool.tile([P, CHUNK], BF16, name="grpat", align_bytes=64)
-                piece = 2 * r + h
-                regroup("g", raw_a[a], grpa[a], 64, 4 * piece, 4 * piece + 4)
-            if h == 0 and k % 3 == 0 and 1 <= k // 3 <= 4:
-                quantise(grpa[k // 3], cod_a[k // 3], sca_a[k // 3])
-            if h == 1 and k + 1 < 16:
-                cod0[k + 1] = cod0_pool.tile([P, CHUNK // 4], U32, name="cod0t", align_bytes=64)
-                sca0[k + 1] = cod0_pool.tile([P, CHUNK // 4], U8, name="sca0t", align_bytes=64)
-                quantise(grp0[k + 1], cod0[k + 1], sca0[k + 1])
-            banks = []
+            if t == 0:
+                load_a(3)
+                load_b(1)
+            if t % 2 == 0 and t // 2 + 4 < 16:
+                load_a(t // 2 + 4)
+            if t in (4, 10, 16):
+                load_b(2 + (t - 4) // 6)
+            if t == 3:
+                nc.vector.quantize_mx(out=cod_b[0][:, BANK : 2 * BANK].bitcast(FP8X4), scales=sca_b[0][:, BANK : 2 * BANK], in_=grp2[1][:])
+            if t + 1 < STEPS:
+                quantise_a(t + 1)
+            if (t - 1) in b_step:
+                quantise_b(b_step[t - 1])
+            if t == 0:
+                regroup_a(2, SPLIT_P, "v")
+            if t == 2:
+                grp2[1] = grpb_pool.tile([P, HALF], BF16, name="grp2t", align_bytes=64)
+                regroup3(raw_b[0][:, 16:32, :], grp2[1][:], 32, SPLIT_P2, "v")
+            for e in "vg":
+                if t + 3 < STEPS:
+                    regroup_a(t + 3, SPLIT_A, e)
+                if t in b_step:
+                    regroup_b(b_step[t], SPLIT_B, e)
             for i in range(TILES):
-                bank = ps_b0.tile([P, BANK], F32, name="bank_0")
-                mx_pass(bank, i, cod0[k], sca0[k], h)
-                banks.append(bank)
-            for i in range(TILES):
-                prod[(t, i)] = prod_pool.tile([P, BANK], F32, name="prodt")
+                bank_a[i] = ps_a.tile([P, BANK], F32, name="bank_a")
+                mx_pass(bank_a[i], i, cod_a[t][:], sca_a[t][:])
+            for pair in range(2):
                 for q in range(4):
-                    u = 8 * k + 4 * h + q
-                    nc.scalar.activation(
-                        out=prod[(t, i)][:, P * q : P * (q + 1)],
-                        in_=banks[i][:, P * q : P * (q + 1)],
-                        func=ACT.Copy,
-                        scale=xs[:, i, u : u + 1],
-                    )
-            for n in range(2 - h):
-                do_unit(next_unit)
-                next_unit += 1
-            if t > 0:
-                transposes(t - 1)
-        transposes(STEPS - 1)
+                    for i in (2 * pair, 2 * pair + 1):
+                        u = 4 * t + q
+                        nc.vector.scalar_tensor_tensor(
+                            out=fin[:, i, 0:128],
+                            in0=bank_a[i][:, P * q : P * (q + 1)],
+                            scalar=xs[:, i, u : u + 1],
+                            in1=fin[:, i, 0:128],
+                            op0=ALU.mult,
+                            op1=ALU.add,
+                        )
+            for j in range(unit_lo(t), unit_lo(t + 1)):
+                n, part = units[j]
+                if part == 0 and j > 0 and next_bank < len(b_banks):
+                    b_pass(next_bank)
+                    next_bank += 1
+                if j == 33:
+                    evacuate(0, "ss")
+                if j - LAG >= 0:
+                    unit_sums(j - LAG)
+                unit_products(j)
+                if j == unit_lo(t):
+                    if t == 0:
+                        regroup_a(2, SPLIT_P, "s")
+                    if t == 2:
+                        regroup3(raw_b[0][:, 16:32, :], grp2[1][:], 32, SPLIT_P2, "s")
+                    if t + 3 < STEPS:
+                        regroup_a(t + 3, SPLIT_A, "s")
+                    if t in b_step:
+                        regroup_b(b_step[t], SPLIT_B, "s")
+        for j in range(96 - LAG, 96):
+            unit_sums(j)
 
-        out_v = out.rearrange("(i g) c -> g i c", g=P)
-        nc.vector.tensor_tensor(
-            out=fin[:, :, 128:320].rearrange("p i (c m) -> p i c m", m=3),
-            in0=acc1[:, :, 0].rearrange("p i m c -> p i c m"),
-            in1=acc1[:, :, 1].rearrange("p i m c -> p i c m"),
-            op=ALU.add,
-        )
-        nc.vector.tensor_tensor(
-            out=fin[:, :, 320:480].rearrange("p i (c m) -> p i c m", m=5),
-            in0=acc2[:, :, 0].rearrange("p i m c -> p i c m"),
-            in1=acc2[:, :, 1].rearrange("p i m c -> p i c m"),
-            op=ALU.add,
-        )
-        nc.sync.dma_start(out=out_v[:, :, 128:480], in_=fin[:, :, 128:480])
-        nc.scalar.copy(out=ot_sb[:], in_=o_t[:])
-        back = ps_b0.tile([P, BANK], F32, name="bank_0")
-        for i in range(TILES):
-            nc.tensor.transpose(out=back[:, P * i : P * (i + 1)], in_=ot_sb[:, P * i : P * (i + 1)], identity=ident[:])
-        nc.scalar.copy(out=fin[:, :, 0:128], in_=back[:].rearrange("p (i c) -> p i c", i=TILES))
         nc.sync.dma_start(out=out_v[:, :, 0:128], in_=fin[:, :, 0:128])
+        evacuate(1, "sv")
+        finish(0, ps_a, "bank_a", "vv")
+        nc.sync.dma_start(out=out_v[:, :, 320:480], in_=fin[:, :, 320:480])
+        finish(1, ps_b, "bank_b", "sv")
+        nc.sync.dma_start(out=out_v[:, :, 128:320], in_=fin[:, :, 128:320])

@@ -54,6 +54,7 @@ def tile_selfconnectionintro_kernel(tc, x, z, w0, w1, w2, out):
         zq = const.tile([P, N], U32, name="zq", align_bytes=64)
         zs = const.tile([P, N], U8, name="zs", align_bytes=64)
         fin = const.tile([P, TILES, DX], F32, name="fin")
+        acc0 = const.tile([P, 2, TILES, P], F32, name="acc0")
         raw_b = [const.tile([P, 32, 128], BF16, name="raw_b0")]
         for a in range(4):
             raw_b.append(const.tile([P, 16, 256], BF16, name="raw_b%d" % (a + 1)))
@@ -146,7 +147,7 @@ def tile_selfconnectionintro_kernel(tc, x, z, w0, w1, w2, out):
         load_b(0, 16, 32)
 
         make_identity(nc, ident[:])
-        nc.vector.memset(fin[:, :, 0:128], 0.0)
+        nc.vector.memset(acc0[:], 0.0)
         perm = []
         fold = []
         for mul in (32, 64):
@@ -337,10 +338,10 @@ def tile_selfconnectionintro_kernel(tc, x, z, w0, w1, w2, out):
                     for i in (2 * pair, 2 * pair + 1):
                         u = 4 * t + q
                         nc.vector.scalar_tensor_tensor(
-                            out=fin[:, i, 0:128],
+                            out=acc0[:, q % 2, i, :],
                             in0=bank_a[i][:, P * q : P * (q + 1)],
                             scalar=xs[:, i, u : u + 1],
-                            in1=fin[:, i, 0:128],
+                            in1=acc0[:, q % 2, i, :],
                             op0=ALU.mult,
                             op1=ALU.add,
                         )
@@ -366,6 +367,7 @@ def tile_selfconnectionintro_kernel(tc, x, z, w0, w1, w2, out):
         for j in range(96 - LAG, 96):
             unit_sums(j)
 
+        nc.vector.tensor_tensor(out=fin[:, :, 0:128], in0=acc0[:, 0], in1=acc0[:, 1], op=ALU.add)
         nc.sync.dma_start(out=out_v[:, :, 0:128], in_=fin[:, :, 0:128])
         evacuate(1, "sv")
         finish(0, ps_a, "bank_a", "vv")

@@ -23,13 +23,13 @@ FLOPS = 2 * N * V * (128 * 128 + 64 * 64 + 32 * 32) + 2 * N * (128 * 128 + 64 * 
 
 STEPS = 32
 SPLIT_A = (96, 32, 0)
-SPLIT_B = (0, 48, 16)
+SPLIT_B = (0, 64, 0)
 SPLIT_P = (0, 88, 40)
 SPLIT_P2 = (0, 20, 12)
 B_OFF = 3
 B_NUM, B_DEN = 3, 2
 LAG = 1
-U_NUM, U_DEN = 3, 1
+U_W2, U_W1, U_STEP = 16, 13, 42
 
 
 def tile_selfconnectionintro_kernel(tc, x, z, w0, w1, w2, out):
@@ -180,14 +180,14 @@ def tile_selfconnectionintro_kernel(tc, x, z, w0, w1, w2, out):
         nc.vector.tensor_copy(out=zgf[:, 0], in_=zts[0][:].rearrange("p i u g -> p i g u"))
         nc.vector.quantize_mx(out=cod_b[0][:, 0:BANK].bitcast(FP8X4), scales=sca_b[0][:, 0:BANK], in_=grp2[0][:])
         nc.scalar.activation(out=xs[:, :, 320:480], in_=x_sb[:, :, 320:480], func=ACT.Copy, scale=1.0 / 128.0)
+        nc.vector.tensor_scalar(
+            out=xs[:, :, 128:320], in0=x_sb[:, :, 128:320], scalar1=1.0 / (64.0 * 512.0) ** 0.5, scalar2=0.0, op0=ALU.mult, op1=ALU.add
+        )
         nc.scalar.copy(out=zgf[:, 1], in_=zts[1][:].rearrange("p i u g -> p i g u"))
         nc.gpsimd.tensor_scalar(out=xs[:, :, 0:128], in0=x_sb[:, :, 0:128], scalar1=1.0 / 256.0, scalar2=0.0, op0=ALU.mult, op1=ALU.add)
         regroup_a(0, SPLIT_P, "vs")
         quantise(zg[:], zq[:], zs[:])
         quantise_a(0)
-        nc.gpsimd.tensor_scalar(
-            out=xs[:, :, 128:320], in0=x_sb[:, :, 128:320], scalar1=1.0 / (64.0 * 512.0) ** 0.5, scalar2=0.0, op0=ALU.mult, op1=ALU.add
-        )
 
         b_banks = [(a, h, i) for a in range(5) for h in range(2) for i in range(TILES)]
         units = []
@@ -291,6 +291,9 @@ def tile_selfconnectionintro_kernel(tc, x, z, w0, w1, w2, out):
                     nc.vector.tensor_copy(
                         out=fin[:, 2 * b : 2 * b + 2, off : off + mul * d], in_=b_ps[:].rearrange("p i c m -> p i (c m)")
                     )
+                nc.sync.dma_start(
+                    out=out_v[:, 2 * b : 2 * b + 2, off : off + mul * d], in_=fin[:, 2 * b : 2 * b + 2, off : off + mul * d]
+                )
 
         b_pass(0)
         b_pass(1)
@@ -298,7 +301,8 @@ def tile_selfconnectionintro_kernel(tc, x, z, w0, w1, w2, out):
         regroup_a(1, SPLIT_P, "vs")
 
         def unit_lo(t):
-            return min(96, (U_NUM * t) // U_DEN)
+            budget = U_STEP * t
+            return min(32, budget // U_W2) + min(64, max(0, budget - 32 * U_W2) // U_W1)
 
         b_step = {}
         for m in range(16):
@@ -371,6 +375,4 @@ def tile_selfconnectionintro_kernel(tc, x, z, w0, w1, w2, out):
         nc.sync.dma_start(out=out_v[:, :, 0:128], in_=fin[:, :, 0:128])
         evacuate(1, "sv")
         finish(0, ps_a, "bank_a", "vv")
-        nc.sync.dma_start(out=out_v[:, :, 320:480], in_=fin[:, :, 320:480])
         finish(1, ps_b, "bank_b", "sv")
-        nc.sync.dma_start(out=out_v[:, :, 128:320], in_=fin[:, :, 128:320])

@@ -22,14 +22,14 @@ HALF = 2048
 FLOPS = 2 * N * V * (128 * 128 + 64 * 64 + 32 * 32) + 2 * N * (128 * 128 + 64 * 64 * 3 + 32 * 32 * 5)
 
 STEPS = 32
-SPLIT_A = (96, 32, 0)
-SPLIT_B = (0, 64, 0)
+SPLIT_A = (100, 28, 0)
+SPLIT_B = (0, 32, 32)
 SPLIT_P = (0, 88, 40)
 SPLIT_P2 = (0, 20, 12)
 B_OFF = 3
 B_NUM, B_DEN = 3, 2
 LAG = 1
-U_W2, U_W1, U_STEP = 16, 13, 42
+U_NUM, U_DEN = 3, 1
 
 
 def tile_selfconnectionintro_kernel(tc, x, z, w0, w1, w2, out):
@@ -180,14 +180,14 @@ def tile_selfconnectionintro_kernel(tc, x, z, w0, w1, w2, out):
         nc.vector.tensor_copy(out=zgf[:, 0], in_=zts[0][:].rearrange("p i u g -> p i g u"))
         nc.vector.quantize_mx(out=cod_b[0][:, 0:BANK].bitcast(FP8X4), scales=sca_b[0][:, 0:BANK], in_=grp2[0][:])
         nc.scalar.activation(out=xs[:, :, 320:480], in_=x_sb[:, :, 320:480], func=ACT.Copy, scale=1.0 / 128.0)
-        nc.vector.tensor_scalar(
-            out=xs[:, :, 128:320], in0=x_sb[:, :, 128:320], scalar1=1.0 / (64.0 * 512.0) ** 0.5, scalar2=0.0, op0=ALU.mult, op1=ALU.add
-        )
         nc.scalar.copy(out=zgf[:, 1], in_=zts[1][:].rearrange("p i u g -> p i g u"))
         nc.gpsimd.tensor_scalar(out=xs[:, :, 0:128], in0=x_sb[:, :, 0:128], scalar1=1.0 / 256.0, scalar2=0.0, op0=ALU.mult, op1=ALU.add)
         regroup_a(0, SPLIT_P, "vs")
         quantise(zg[:], zq[:], zs[:])
         quantise_a(0)
+        nc.gpsimd.tensor_scalar(
+            out=xs[:, :, 128:320], in0=x_sb[:, :, 128:320], scalar1=1.0 / (64.0 * 512.0) ** 0.5, scalar2=0.0, op0=ALU.mult, op1=ALU.add
+        )
 
         b_banks = [(a, h, i) for a in range(5) for h in range(2) for i in range(TILES)]
         units = []
@@ -291,9 +291,6 @@ def tile_selfconnectionintro_kernel(tc, x, z, w0, w1, w2, out):
                     nc.vector.tensor_copy(
                         out=fin[:, 2 * b : 2 * b + 2, off : off + mul * d], in_=b_ps[:].rearrange("p i c m -> p i (c m)")
                     )
-                nc.sync.dma_start(
-                    out=out_v[:, 2 * b : 2 * b + 2, off : off + mul * d], in_=fin[:, 2 * b : 2 * b + 2, off : off + mul * d]
-                )
 
         b_pass(0)
         b_pass(1)
@@ -301,8 +298,7 @@ def tile_selfconnectionintro_kernel(tc, x, z, w0, w1, w2, out):
         regroup_a(1, SPLIT_P, "vs")
 
         def unit_lo(t):
-            budget = U_STEP * t
-            return min(32, budget // U_W2) + min(64, max(0, budget - 32 * U_W2) // U_W1)
+            return min(96, (U_NUM * t) // U_DEN)
 
         b_step = {}
         for m in range(16):
@@ -375,4 +371,6 @@ def tile_selfconnectionintro_kernel(tc, x, z, w0, w1, w2, out):
         nc.sync.dma_start(out=out_v[:, :, 0:128], in_=fin[:, :, 0:128])
         evacuate(1, "sv")
         finish(0, ps_a, "bank_a", "vv")
+        nc.sync.dma_start(out=out_v[:, :, 320:480], in_=fin[:, :, 320:480])
         finish(1, ps_b, "bank_b", "sv")
+        nc.sync.dma_start(out=out_v[:, :, 128:320], in_=fin[:, :, 128:320])

@@ -148,22 +148,11 @@ def tile_selfconnectionintro_kernel(tc, x, z, w0, w1, w2, out):
 
         make_identity(nc, ident[:])
         nc.vector.memset(acc0[:], 0.0)
-        perm = []
-        fold = []
-        for mul in (32, 64):
-            pm = const.tile([P, P], F32, name="perm%d" % mul)
-            nc.gpsimd.tensor_scalar(
-                out=pm[:].rearrange("p (c m) -> p c m", c=mul),
-                in0=ident[:].rearrange("p (m c) -> p c m", c=mul),
-                scalar1=1.0,
-                scalar2=0.0,
-                op0=ALU.mult,
-                op1=ALU.add,
-            )
-            perm.append(pm)
-            sm = const.tile([P, mul], F32, name="fold%d" % mul)
-            nc.vector.tensor_reduce(out=sm[:], in_=ident[:].rearrange("p (q c) -> p c q", c=mul), axis=mybir.AxisListType.X, op=ALU.add)
-            fold.append(sm)
+        fold64 = const.tile([P, 64], F32, name="fold64")
+        nc.gpsimd.tensor_tensor(out=fold64[:], in0=ident[:, 0:64], in1=ident[:, 64:128], op=ALU.add)
+        fold32 = const.tile([P, 32], F32, name="fold32")
+        nc.gpsimd.tensor_tensor(out=fold32[:], in0=fold64[:, 0:32], in1=fold64[:, 32:64], op=ALU.add)
+        fold = [fold32, fold64]
 
         zw = z_sb[:].bitcast(F32).rearrange("g (i p u) -> g i u p", i=TILES, u=2)
         zgf = zg[:].bitcast(F32).rearrange("p (b i g u) -> p b i g u", b=2, i=2, u=2)
@@ -174,16 +163,16 @@ def tile_selfconnectionintro_kernel(tc, x, z, w0, w1, w2, out):
                 for u in range(2):
                     nc.tensor.transpose(out=zt[:, ii, u, :], in_=zw[:, 2 * b + ii, u, :], identity=ident[:])
             zts.append(zt)
+        nc.vector.tensor_copy(out=zgf[:, 0], in_=zts[0][:].rearrange("p i u g -> p i g u"))
+        nc.scalar.copy(out=zgf[:, 1], in_=zts[1][:].rearrange("p i u g -> p i g u"))
+        quantise(zg[:], zq[:], zs[:])
         grp2 = {}
         grp2[0] = grpb_pool.tile([P, HALF], BF16, name="grp2t", align_bytes=64)
         regroup3(raw_b[0][:, 0:16, :], grp2[0][:], 32, SPLIT_P2, "vs")
-        nc.vector.tensor_copy(out=zgf[:, 0], in_=zts[0][:].rearrange("p i u g -> p i g u"))
-        nc.vector.quantize_mx(out=cod_b[0][:, 0:BANK].bitcast(FP8X4), scales=sca_b[0][:, 0:BANK], in_=grp2[0][:])
         nc.scalar.activation(out=xs[:, :, 320:480], in_=x_sb[:, :, 320:480], func=ACT.Copy, scale=1.0 / 128.0)
-        nc.scalar.copy(out=zgf[:, 1], in_=zts[1][:].rearrange("p i u g -> p i g u"))
+        nc.vector.quantize_mx(out=cod_b[0][:, 0:BANK].bitcast(FP8X4), scales=sca_b[0][:, 0:BANK], in_=grp2[0][:])
         nc.gpsimd.tensor_scalar(out=xs[:, :, 0:128], in0=x_sb[:, :, 0:128], scalar1=1.0 / 256.0, scalar2=0.0, op0=ALU.mult, op1=ALU.add)
         regroup_a(0, SPLIT_P, "vs")
-        quantise(zg[:], zq[:], zs[:])
         quantise_a(0)
         nc.gpsimd.tensor_scalar(
             out=xs[:, :, 128:320], in0=x_sb[:, :, 128:320], scalar1=1.0 / (64.0 * 512.0) ** 0.5, scalar2=0.0, op0=ALU.mult, op1=ALU.add
@@ -254,48 +243,42 @@ def tile_selfconnectionintro_kernel(tc, x, z, w0, w1, w2, out):
 
         t_sb = {}
 
-        def evacuate(blk, engines):
+        def evacuate(blk, engines, pieces):
             for kd in range(2):
                 t_sb[(blk, kd)] = const.tile([P, N], F32, name="t_sb%d%d" % (blk, kd))
-                if engines[kd] == "s":
-                    nc.scalar.copy(out=t_sb[(blk, kd)][:], in_=acc_t[blk][kd][:])
-                else:
-                    nc.vector.tensor_copy(out=t_sb[(blk, kd)][:], in_=acc_t[blk][kd][:])
+            w = N // pieces
+            for g in range(pieces):
+                for kd in range(2):
+                    if engines[kd] == "s":
+                        nc.scalar.copy(out=t_sb[(blk, kd)][:, w * g : w * (g + 1)], in_=acc_t[blk][kd][:, w * g : w * (g + 1)])
+                    else:
+                        nc.vector.tensor_copy(out=t_sb[(blk, kd)][:, w * g : w * (g + 1)], in_=acc_t[blk][kd][:, w * g : w * (g + 1)])
 
         def finish(blk, pool, tag, copier):
             mul, d, off = (32, 5, 320) if blk == 0 else (64, 3, 128)
-            full = P // mul
             for b in range(2):
-                b_ps = pool.tile([P, 2, mul, d], F32, name=tag)
+                b_ps = pool.tile([P, 2, d * mul], F32, name=tag)
                 for ii in range(2):
                     i = 2 * b + ii
+                    nc.tensor.transpose(out=b_ps[:, ii, 0:P], in_=t_sb[(blk, 0)][:, P * i : P * (i + 1)], identity=ident[:])
                     nc.tensor.matmul(
-                        out=b_ps[:, ii, :, 0:full],
-                        lhsT=t_sb[(blk, 0)][:, P * i : P * (i + 1)],
-                        rhs=perm[blk][:],
-                        start=True,
-                        stop=True,
-                    )
-                    nc.tensor.matmul(
-                        out=b_ps[:, ii, :, full],
+                        out=b_ps[:, ii, P : P + mul],
                         lhsT=t_sb[(blk, 1)][:, P * i : P * (i + 1)],
                         rhs=fold[blk][:],
                         start=True,
                         stop=True,
                     )
+                dst = fin[:, 2 * b : 2 * b + 2, off : off + mul * d].rearrange("p i (c m) -> p i c m", m=d)
                 if copier[b] == "s":
-                    nc.scalar.copy(
-                        out=fin[:, 2 * b : 2 * b + 2, off : off + mul * d], in_=b_ps[:].rearrange("p i c m -> p i (c m)")
-                    )
+                    nc.scalar.copy(out=dst, in_=b_ps[:].rearrange("p i (m c) -> p i c m", c=mul))
                 else:
-                    nc.vector.tensor_copy(
-                        out=fin[:, 2 * b : 2 * b + 2, off : off + mul * d], in_=b_ps[:].rearrange("p i c m -> p i (c m)")
-                    )
+                    nc.vector.tensor_copy(out=dst, in_=b_ps[:].rearrange("p i (m c) -> p i c m", c=mul))
+                nc.sync.dma_start(out=out_v[:, 2 * b : 2 * b + 2, off : off + mul * d], in_=fin[:, 2 * b : 2 * b + 2, off : off + mul * d])
 
         b_pass(0)
         b_pass(1)
-        next_bank = 2
-        regroup_a(1, SPLIT_P, "vs")
+        state = {"bank": 2}
+        regroup_a(1, SPLIT_P, "v")
 
         def unit_lo(t):
             return min(96, (U_NUM * t) // U_DEN)
@@ -306,14 +289,7 @@ def tile_selfconnectionintro_kernel(tc, x, z, w0, w1, w2, out):
         out_v = out.rearrange("(i g) c -> g i c", g=P)
         bank_a = {}
 
-        for t in range(STEPS):
-            if t == 0:
-                load_a(3)
-                load_b(1)
-            if t % 2 == 0 and t // 2 + 4 < 16:
-                load_a(t // 2 + 4)
-            if t in (4, 10, 16):
-                load_b(2 + (t - 4) // 6)
+        def port_work(t):
             if t == 3:
                 nc.vector.quantize_mx(out=cod_b[0][:, BANK : 2 * BANK].bitcast(FP8X4), scales=sca_b[0][:, BANK : 2 * BANK], in_=grp2[1][:])
             if t + 1 < STEPS:
@@ -330,47 +306,67 @@ def tile_selfconnectionintro_kernel(tc, x, z, w0, w1, w2, out):
                     regroup_a(t + 3, SPLIT_A, e)
                 if t in b_step:
                     regroup_b(b_step[t], SPLIT_B, e)
+
+        def macs(t, pair):
+            for q in range(4):
+                for i in (2 * pair, 2 * pair + 1):
+                    u = 4 * t + q
+                    nc.vector.scalar_tensor_tensor(
+                        out=acc0[:, q % 2, i, :],
+                        in0=bank_a[i][:, P * q : P * (q + 1)],
+                        scalar=xs[:, i, u : u + 1],
+                        in1=acc0[:, q % 2, i, :],
+                        op0=ALU.mult,
+                        op1=ALU.add,
+                    )
+
+        def unit(j, t):
+            n, part = units[j]
+            if part == 0 and j > 0 and state["bank"] < len(b_banks):
+                b_pass(state["bank"])
+                state["bank"] = state["bank"] + 1
+            if j == 33:
+                evacuate(0, "ss", 1)
+            if j - LAG >= 0:
+                unit_sums(j - LAG)
+            unit_products(j)
+            if j < 2:
+                regroup_a(j + 1, SPLIT_P, "s")
+            if j == max(unit_lo(t), 1):
+                if t == 2:
+                    regroup3(raw_b[0][:, 16:32, :], grp2[1][:], 32, SPLIT_P2, "s")
+                if t + 3 < STEPS:
+                    regroup_a(t + 3, SPLIT_A, "s")
+                if t in b_step:
+                    regroup_b(b_step[t], SPLIT_B, "s")
+
+        for t in range(STEPS):
+            if t == 0:
+                load_a(3)
+                load_b(1)
+            if t % 2 == 0 and t // 2 + 4 < 16:
+                load_a(t // 2 + 4)
+            if t in (4, 10, 16):
+                load_b(2 + (t - 4) // 6)
+            if t > 0:
+                port_work(t)
             for i in range(TILES):
                 bank_a[i] = ps_a.tile([P, BANK], F32, name="bank_a")
                 mx_pass(bank_a[i], i, cod_a[t][:], sca_a[t][:])
-            for pair in range(2):
-                for q in range(4):
-                    for i in (2 * pair, 2 * pair + 1):
-                        u = 4 * t + q
-                        nc.vector.scalar_tensor_tensor(
-                            out=acc0[:, q % 2, i, :],
-                            in0=bank_a[i][:, P * q : P * (q + 1)],
-                            scalar=xs[:, i, u : u + 1],
-                            in1=acc0[:, q % 2, i, :],
-                            op0=ALU.mult,
-                            op1=ALU.add,
-                        )
-            for j in range(unit_lo(t), unit_lo(t + 1)):
-                n, part = units[j]
-                if part == 0 and j > 0 and next_bank < len(b_banks):
-                    b_pass(next_bank)
-                    next_bank += 1
-                if j == 33:
-                    evacuate(0, "ss")
-                if j - LAG >= 0:
-                    unit_sums(j - LAG)
-                unit_products(j)
-                if j == unit_lo(t):
-                    if t == 0:
-                        regroup_a(2, SPLIT_P, "s")
-                    if t == 2:
-                        regroup3(raw_b[0][:, 16:32, :], grp2[1][:], 32, SPLIT_P2, "s")
-                    if t + 3 < STEPS:
-                        regroup_a(t + 3, SPLIT_A, "s")
-                    if t in b_step:
-                        regroup_b(b_step[t], SPLIT_B, "s")
+            macs(t, 0)
+            first = unit_lo(t)
+            if t == 0:
+                unit(0, 0)
+                first = 1
+                port_work(0)
+            macs(t, 1)
+            for j in range(first, unit_lo(t + 1)):
+                unit(j, t)
         for j in range(96 - LAG, 96):
             unit_sums(j)
 
-        nc.vector.tensor_tensor(out=fin[:, :, 0:128], in0=acc0[:, 0], in1=acc0[:, 1], op=ALU.add)
+        nc.gpsimd.tensor_tensor(out=fin[:, :, 0:128], in0=acc0[:, 0], in1=acc0[:, 1], op=ALU.add)
         nc.sync.dma_start(out=out_v[:, :, 0:128], in_=fin[:, :, 0:128])
-        evacuate(1, "sv")
-        finish(0, ps_a, "bank_a", "vv")
-        nc.sync.dma_start(out=out_v[:, :, 320:480], in_=fin[:, :, 320:480])
+        evacuate(1, "sv", 2)
+        finish(0, ps_a, "bank_a", "sv")
         finish(1, ps_b, "bank_b", "sv")
-        nc.sync.dma_start(out=out_v[:, :, 128:320], in_=fin[:, :, 128:320])

@@ -277,7 +277,7 @@ def tile_selfconnectionintro_kernel(tc, x, z, w0, w1, w2, out):
 
         b_pass(0)
         b_pass(1)
-        state = {"bank": 2}
+        state = {"bank": 2, "deferred": False}
         regroup_a(1, SPLIT_P, "v")
 
         def unit_lo(t):
@@ -323,8 +323,12 @@ def tile_selfconnectionintro_kernel(tc, x, z, w0, w1, w2, out):
         def unit(j, t):
             n, part = units[j]
             if part == 0 and j > 0 and state["bank"] < len(b_banks):
-                b_pass(state["bank"])
-                state["bank"] = state["bank"] + 1
+                per_bank = 4 if b_banks[n][0] == 0 else 2
+                if j > unit_lo(t) and j + per_bank > unit_lo(t + 1):
+                    state["deferred"] = True
+                else:
+                    b_pass(state["bank"])
+                    state["bank"] = state["bank"] + 1
             if j == 33:
                 evacuate(0, "ss", 1)
             if j - LAG >= 0:
@@ -350,6 +354,10 @@ def tile_selfconnectionintro_kernel(tc, x, z, w0, w1, w2, out):
                 load_b(2 + (t - 4) // 6)
             if t > 0:
                 port_work(t)
+            if state["deferred"]:
+                b_pass(state["bank"])
+                state["bank"] = state["bank"] + 1
+                state["deferred"] = False
             for i in range(TILES):
                 bank_a[i] = ps_a.tile([P, BANK], F32, name="bank_a")
                 mx_pass(bank_a[i], i, cod_a[t][:], sca_a[t][:])

@@ -66,13 +66,12 @@ def tile_selfconnectionintro_kernel(tc, x, z, w0, w1, w2, out):
                 return
             dst = grp.rearrange("p (u c j) -> p u c j", c=mul, j=4)[:, :, c0:c1, :]
             src = raw.rearrange("p u (j c) -> p u c j", j=4)[:, :, c0:c1, :]
+            dst4 = grp.rearrange("p (u c i j) -> p u c j i", c=mul // 4, i=4, j=4)[:, :, c0 // 4 : c1 // 4, :, :]
+            src4 = raw.rearrange("p u (j c i) -> p u c j i", j=4, i=4)[:, :, c0 // 4 : c1 // 4, :, :]
             if eng == "v":
-                nc.vector.tensor_copy(
-                    out=grp.rearrange("p (u c i j) -> p u c j i", c=mul // 4, i=4, j=4)[:, :, c0 // 4 : c1 // 4, :, :],
-                    in_=raw.rearrange("p u (j c i) -> p u c j i", j=4, i=4)[:, :, c0 // 4 : c1 // 4, :, :],
-                )
+                nc.vector.tensor_copy(out=dst4, in_=src4)
             elif eng == "s":
-                nc.scalar.copy(out=dst, in_=src)
+                nc.scalar.copy(out=dst4, in_=src4)
             else:
                 nc.gpsimd.tensor_scalar(out=dst, in0=src, scalar1=1.0, scalar2=0.0, op0=ALU.mult, op1=ALU.add)
 
@@ -105,9 +104,10 @@ def tile_selfconnectionintro_kernel(tc, x, z, w0, w1, w2, out):
         cod_a = {}
         sca_a = {}
 
-        def load_a(k, halves=False):
-            raw_a[k] = raw_pool.tile([P, 8, 512], BF16, name="rawt")
-            for lo, hi in ((0, 4), (4, 8)) if halves else ((0, 8),):
+        def load_a(k, parts=((0, 8),)):
+            if k not in raw_a:
+                raw_a[k] = raw_pool.tile([P, 8, 512], BF16, name="rawt")
+            for lo, hi in parts:
                 nc.sync.dma_start(
                     out=raw_a[k][:, lo:hi, :], in_=w0[8 * k + lo : 8 * k + hi].rearrange("u (p j) c -> p u (j c)", j=4)
                 )
@@ -139,10 +139,14 @@ def tile_selfconnectionintro_kernel(tc, x, z, w0, w1, w2, out):
             quantise(grp_b[m][:], cod_b[a][:, 256 * r : 256 * (r + 1)], sca_b[a][:, 256 * r : 256 * (r + 1)])
 
         nc.sync.dma_start(out=z_sb[:].rearrange("g (i v) -> g i v", i=TILES), in_=z.rearrange("(i g) v -> g i v", g=P))
+        x_v = x.rearrange("(i g) c -> g i c", g=P)
+        load_a(0, ((0, 4),))
+        nc.sync.dma_start(out=x_sb[:, :, 0:128], in_=x_v[:, :, 0:128])
         load_b(0, 0, 16)
-        nc.sync.dma_start(out=x_sb[:], in_=x.rearrange("(i g) c -> g i c", g=P))
-        load_a(0, True)
-        load_a(1, True)
+        nc.sync.dma_start(out=x_sb[:, :, 320:480], in_=x_v[:, :, 320:480])
+        load_a(0, ((4, 8),))
+        load_a(1, ((0, 4), (4, 8)))
+        nc.sync.dma_start(out=x_sb[:, :, 128:320], in_=x_v[:, :, 128:320])
         load_a(2)
         load_b(0, 16, 32)
 
@@ -165,15 +169,15 @@ def tile_selfconnectionintro_kernel(tc, x, z, w0, w1, w2, out):
             zts.append(zt)
         nc.vector.tensor_copy(out=zgf[:, 0], in_=zts[0][:].rearrange("p i u g -> p i g u"))
         nc.scalar.copy(out=zgf[:, 1], in_=zts[1][:].rearrange("p i u g -> p i g u"))
+        regroup_a(0, SPLIT_P, "vs")
         quantise(zg[:], zq[:], zs[:])
+        nc.gpsimd.tensor_scalar(out=xs[:, :, 0:128], in0=x_sb[:, :, 0:128], scalar1=1.0 / 256.0, scalar2=0.0, op0=ALU.mult, op1=ALU.add)
+        quantise_a(0)
         grp2 = {}
         grp2[0] = grpb_pool.tile([P, HALF], BF16, name="grp2t", align_bytes=64)
         regroup3(raw_b[0][:, 0:16, :], grp2[0][:], 32, SPLIT_P2, "vs")
         nc.scalar.activation(out=xs[:, :, 320:480], in_=x_sb[:, :, 320:480], func=ACT.Copy, scale=1.0 / 128.0)
         nc.vector.quantize_mx(out=cod_b[0][:, 0:BANK].bitcast(FP8X4), scales=sca_b[0][:, 0:BANK], in_=grp2[0][:])
-        nc.gpsimd.tensor_scalar(out=xs[:, :, 0:128], in0=x_sb[:, :, 0:128], scalar1=1.0 / 256.0, scalar2=0.0, op0=ALU.mult, op1=ALU.add)
-        regroup_a(0, SPLIT_P, "vs")
-        quantise_a(0)
         nc.gpsimd.tensor_scalar(
             out=xs[:, :, 128:320], in0=x_sb[:, :, 128:320], scalar1=1.0 / (64.0 * 512.0) ** 0.5, scalar2=0.0, op0=ALU.mult, op1=ALU.add
         )
@@ -275,10 +279,7 @@ def tile_selfconnectionintro_kernel(tc, x, z, w0, w1, w2, out):
                     nc.vector.tensor_copy(out=dst, in_=b_ps[:].rearrange("p i (m c) -> p i c m", c=mul))
                 nc.sync.dma_start(out=out_v[:, 2 * b : 2 * b + 2, off : off + mul * d], in_=fin[:, 2 * b : 2 * b + 2, off : off + mul * d])
 
-        b_pass(0)
-        b_pass(1)
         state = {"bank": 2, "deferred": False}
-        regroup_a(1, SPLIT_P, "v")
 
         def unit_lo(t):
             return min(96, (U_NUM * t) // U_DEN)
@@ -334,8 +335,8 @@ def tile_selfconnectionintro_kernel(tc, x, z, w0, w1, w2, out):
             if j - LAG >= 0:
                 unit_sums(j - LAG)
             unit_products(j)
-            if j < 2:
-                regroup_a(j + 1, SPLIT_P, "s")
+            if j == 0:
+                regroup_a(2, SPLIT_P, "s")
             if j == max(unit_lo(t), 1):
                 if t == 2:
                     regroup3(raw_b[0][:, 16:32, :], grp2[1][:], 32, SPLIT_P2, "s")
@@ -361,14 +362,14 @@ def tile_selfconnectionintro_kernel(tc, x, z, w0, w1, w2, out):
             for i in range(TILES):
                 bank_a[i] = ps_a.tile([P, BANK], F32, name="bank_a")
                 mx_pass(bank_a[i], i, cod_a[t][:], sca_a[t][:])
+                if t == 0 and i % 2 == 1:
+                    b_pass(i // 2)
             macs(t, 0)
-            first = unit_lo(t)
             if t == 0:
-                unit(0, 0)
-                first = 1
+                regroup_a(1, SPLIT_P, "vs")
                 port_work(0)
             macs(t, 1)
-            for j in range(first, unit_lo(t + 1)):
+            for j in range(unit_lo(t), unit_lo(t + 1)):
                 unit(j, t)
         for j in range(96 - LAG, 96):
             unit_sums(j)

@@ -23,7 +23,7 @@ FLOPS = 2 * N * V * (128 * 128 + 64 * 64 + 32 * 32) + 2 * N * (128 * 128 + 64 * 
 
 STEPS = 32
 SPLIT_A = (100, 28, 0)
-SPLIT_B = (0, 32, 32)
+SPLIT_B = (0, 28, 36)
 SPLIT_P = (0, 88, 40)
 SPLIT_P2 = (0, 20, 12)
 B_OFF = 3

@@ -22,8 +22,9 @@ HALF = 2048
 FLOPS = 2 * N * V * (128 * 128 + 64 * 64 + 32 * 32) + 2 * N * (128 * 128 + 64 * 64 * 3 + 32 * 32 * 5)
 
 STEPS = 32
-SPLIT_A = (100, 28, 0)
-SPLIT_B = (0, 28, 36)
+SPLIT_A = (112, 16, 0)
+SPLIT_3 = (48, 80, 0)
+SPLIT_B = (0, 36, 28)
 SPLIT_P = (0, 88, 40)
 SPLIT_P2 = (0, 20, 12)
 B_OFF = 3
@@ -304,7 +305,7 @@ def tile_selfconnectionintro_kernel(tc, x, z, w0, w1, w2, out):
                 regroup3(raw_b[0][:, 16:32, :], grp2[1][:], 32, SPLIT_P2, "v")
             for e in "vg":
                 if t + 3 < STEPS:
-                    regroup_a(t + 3, SPLIT_A, e)
+                    regroup_a(t + 3, SPLIT_3 if t == 0 else SPLIT_A, e)
                 if t in b_step:
                     regroup_b(b_step[t], SPLIT_B, e)
 
@@ -341,7 +342,7 @@ def tile_selfconnectionintro_kernel(tc, x, z, w0, w1, w2, out):
                 if t == 2:
                     regroup3(raw_b[0][:, 16:32, :], grp2[1][:], 32, SPLIT_P2, "s")
                 if t + 3 < STEPS:
-                    regroup_a(t + 3, SPLIT_A, "s")
+                    regroup_a(t + 3, SPLIT_3 if t == 0 else SPLIT_A, "s")
                 if t in b_step:
                     regroup_b(b_step[t], SPLIT_B, "s")
 

@@ -25,7 +25,7 @@ STEPS = 32
 SPLIT_A = (112, 16, 0)
 SPLIT_3 = (48, 80, 0)
 SPLIT_B = (0, 36, 28)
-SPLIT_P = (0, 88, 40)
+SPLIT_P = (0, 104, 24)
 SPLIT_P2 = (0, 20, 12)
 B_OFF = 3
 B_NUM, B_DEN = 3, 2
@@ -140,14 +140,12 @@ def tile_selfconnectionintro_kernel(tc, x, z, w0, w1, w2, out):
             quantise(grp_b[m][:], cod_b[a][:, 256 * r : 256 * (r + 1)], sca_b[a][:, 256 * r : 256 * (r + 1)])
 
         nc.sync.dma_start(out=z_sb[:].rearrange("g (i v) -> g i v", i=TILES), in_=z.rearrange("(i g) v -> g i v", g=P))
-        x_v = x.rearrange("(i g) c -> g i c", g=P)
         load_a(0, ((0, 4),))
-        nc.sync.dma_start(out=x_sb[:, :, 0:128], in_=x_v[:, :, 0:128])
-        load_b(0, 0, 16)
-        nc.sync.dma_start(out=x_sb[:, :, 320:480], in_=x_v[:, :, 320:480])
+        load_b(0, 0, 8)
+        load_b(0, 8, 16)
+        nc.sync.dma_start(out=x_sb[:], in_=x.rearrange("(i g) c -> g i c", g=P))
         load_a(0, ((4, 8),))
         load_a(1, ((0, 4), (4, 8)))
-        nc.sync.dma_start(out=x_sb[:, :, 128:320], in_=x_v[:, :, 128:320])
         load_a(2)
         load_b(0, 16, 32)
 
@@ -172,11 +170,15 @@ def tile_selfconnectionintro_kernel(tc, x, z, w0, w1, w2, out):
         nc.scalar.copy(out=zgf[:, 1], in_=zts[1][:].rearrange("p i u g -> p i g u"))
         regroup_a(0, SPLIT_P, "vs")
         quantise(zg[:], zq[:], zs[:])
-        nc.gpsimd.tensor_scalar(out=xs[:, :, 0:128], in0=x_sb[:, :, 0:128], scalar1=1.0 / 256.0, scalar2=0.0, op0=ALU.mult, op1=ALU.add)
+        for b in range(2):
+            nc.gpsimd.tensor_scalar(
+                out=xs[:, 2 * b : 2 * b + 2, 0:128], in0=x_sb[:, 2 * b : 2 * b + 2, 0:128], scalar1=1.0 / 256.0, scalar2=0.0, op0=ALU.mult, op1=ALU.add
+            )
         quantise_a(0)
         grp2 = {}
         grp2[0] = grpb_pool.tile([P, HALF], BF16, name="grp2t", align_bytes=64)
-        regroup3(raw_b[0][:, 0:16, :], grp2[0][:], 32, SPLIT_P2, "vs")
+        for b in range(2):
+            regroup3(raw_b[0][:, 8 * b : 8 * b + 8, :], grp2[0][:, 1024 * b : 1024 * (b + 1)], 32, SPLIT_P2, "vs")
         nc.scalar.activation(out=xs[:, :, 320:480], in_=x_sb[:, :, 320:480], func=ACT.Copy, scale=1.0 / 128.0)
         nc.vector.quantize_mx(out=cod_b[0][:, 0:BANK].bitcast(FP8X4), scales=sca_b[0][:, 0:BANK], in_=grp2[0][:])
         nc.gpsimd.tensor_scalar(
@@ -337,6 +339,7 @@ def tile_selfconnectionintro_kernel(tc, x, z, w0, w1, w2, out):
                 unit_sums(j - LAG)
             unit_products(j)
             if j == 0:
+                regroup_a(1, SPLIT_P, "s")
                 regroup_a(2, SPLIT_P, "s")
             if j == max(unit_lo(t), 1):
                 if t == 2:
@@ -367,10 +370,11 @@ def tile_selfconnectionintro_kernel(tc, x, z, w0, w1, w2, out):
                     b_pass(i // 2)
             macs(t, 0)
             if t == 0:
-                regroup_a(1, SPLIT_P, "vs")
+                regroup_a(1, SPLIT_P, "v")
+                unit(0, 0)
                 port_work(0)
             macs(t, 1)
-            for j in range(unit_lo(t), unit_lo(t + 1)):
+            for j in range(max(unit_lo(t), 1), unit_lo(t + 1)):
                 unit(j, t)
         for j in range(96 - LAG, 96):
             unit_sums(j)

@@ -22,9 +22,9 @@ HALF = 2048
 FLOPS = 2 * N * V * (128 * 128 + 64 * 64 + 32 * 32) + 2 * N * (128 * 128 + 64 * 64 * 3 + 32 * 32 * 5)
 
 STEPS = 32
-SPLIT_A = (112, 16, 0)
+SPLIT_A = (116, 12, 0)
 SPLIT_3 = (48, 80, 0)
-SPLIT_B = (0, 36, 28)
+SPLIT_B = (0, 40, 24)
 SPLIT_P = (0, 104, 24)
 SPLIT_P2 = (0, 20, 12)
 B_OFF = 3
@@ -306,10 +306,10 @@ def tile_selfconnectionintro_kernel(tc, x, z, w0, w1, w2, out):
                 grp2[1] = grpb_pool.tile([P, HALF], BF16, name="grp2t", align_bytes=64)
                 regroup3(raw_b[0][:, 16:32, :], grp2[1][:], 32, SPLIT_P2, "v")
             for e in "vg":
-                if t + 3 < STEPS:
-                    regroup_a(t + 3, SPLIT_3 if t == 0 else SPLIT_A, e)
                 if t in b_step:
                     regroup_b(b_step[t], SPLIT_B, e)
+                if t + 3 < STEPS:
+                    regroup_a(t + 3, SPLIT_3 if t == 0 else SPLIT_A, e)
 
         def macs(t, pair):
             for q in range(4):
@@ -379,7 +379,7 @@ def tile_selfconnectionintro_kernel(tc, x, z, w0, w1, w2, out):
         for j in range(96 - LAG, 96):
             unit_sums(j)
 
-        nc.gpsimd.tensor_tensor(out=fin[:, :, 0:128], in0=acc0[:, 0], in1=acc0[:, 1], op=ALU.add)
+        nc.vector.tensor_tensor(out=fin[:, :, 0:128], in0=acc0[:, 0], in1=acc0[:, 1], op=ALU.add)
         nc.sync.dma_start(out=out_v[:, :, 0:128], in_=fin[:, :, 0:128])
         evacuate(1, "sv", 2)
         finish(0, ps_a, "bank_a", "sv")

@@ -27,7 +27,7 @@ SPLIT_3 = (48, 80, 0)
 SPLIT_B = (0, 40, 24)
 SPLIT_P = (0, 104, 24)
 SPLIT_P2 = (0, 20, 12)
-B_OFF = 3
+B_OFF = 5
 B_NUM, B_DEN = 3, 2
 LAG = 1
 U_NUM, U_DEN = 3, 1

from contextlib import ExitStack

import concourse.mybir as mybir
from concourse.masks import make_identity

F32 = mybir.dt.float32
BF16 = mybir.dt.bfloat16
U32 = mybir.dt.uint32
U8 = mybir.dt.uint8
FP8X4 = mybir.dt.float8_e4m3fn_x4
ALU = mybir.AluOpType
ACT = mybir.ActivationFunctionType

P = 128
N = 512
V = 512
TILES = N // P
DX = 480
BANK = 512
HALF = 2048

FLOPS = 2 * N * V * (128 * 128 + 64 * 64 + 32 * 32) + 2 * N * (128 * 128 + 64 * 64 * 3 + 32 * 32 * 5)

STEPS = 32
SPLIT_A = (116, 12, 0)
SPLIT_3 = (48, 80, 0)
SPLIT_B = (0, 40, 24)
SPLIT_P = (0, 104, 24)
SPLIT_P2 = (0, 20, 12)
B_OFF = 5
B_NUM, B_DEN = 3, 2
LAG = 1
U_NUM, U_DEN = 3, 1


def tile_selfconnectionintro_kernel(tc, x, z, w0, w1, w2, out):
    nc = tc.nc
    with ExitStack() as ctx:
        const = ctx.enter_context(tc.tile_pool(name="const", bufs=1))
        raw_pool = ctx.enter_context(tc.tile_pool(name="raw", bufs=5))
        grpa_pool = ctx.enter_context(tc.tile_pool(name="grpa", bufs=2))
        grpb_pool = ctx.enter_context(tc.tile_pool(name="grpb", bufs=2))
        coda_pool = ctx.enter_context(tc.tile_pool(name="coda", bufs=4))
        prod_pool = ctx.enter_context(tc.tile_pool(name="prod", bufs=6))
        ps_acc = ctx.enter_context(tc.psum_pool(name="psacc", bufs=1))
        ps_a = ctx.enter_context(tc.psum_pool(name="psa", bufs=4))
        ps_b = ctx.enter_context(tc.psum_pool(name="psb", bufs=2))
        ctx.enter_context(tc.manual_schedule())

        ident = const.tile([P, P], F32, name="ident")
        z_sb = const.tile([P, TILES * V], BF16, name="z_sb")
        x_sb = const.tile([P, TILES, DX], BF16, name="x_sb")
        xs = const.tile([P, TILES, DX], F32, name="xs")
        zg = const.tile([P, 4 * N], BF16, name="zg", align_bytes=64)
        zq = const.tile([P, N], U32, name="zq", align_bytes=64)
        zs = const.tile([P, N], U8, name="zs", align_bytes=64)
        fin = const.tile([P, TILES, DX], F32, name="fin")
        acc0 = const.tile([P, 2, TILES, P], F32, name="acc0")
        raw_b = [const.tile([P, 32, 128], BF16, name="raw_b0")]
        for a in range(4):
            raw_b.append(const.tile([P, 16, 256], BF16, name="raw_b%d" % (a + 1)))
        cod_b = [const.tile([P, 1024], U32, name="cod_b%d" % a, align_bytes=64) for a in range(5)]
        sca_b = [const.tile([P, 1024], U8, name="sca_b%d" % a, align_bytes=64) for a in range(5)]

        def regroup(eng, raw, grp, mul, c0, c1):
            if c1 <= c0:
                return
            dst = grp.rearrange("p (u c j) -> p u c j", c=mul, j=4)[:, :, c0:c1, :]
            src = raw.rearrange("p u (j c) -> p u c j", j=4)[:, :, c0:c1, :]
            dst4 = grp.rearrange("p (u c i j) -> p u c j i", c=mul // 4, i=4, j=4)[:, :, c0 // 4 : c1 // 4, :, :]
            src4 = raw.rearrange("p u (j c i) -> p u c j i", j=4, i=4)[:, :, c0 // 4 : c1 // 4, :, :]
            if eng == "v":
                nc.vector.tensor_copy(out=dst4, in_=src4)
            elif eng == "s":
                nc.scalar.copy(out=dst4, in_=src4)
            else:
                nc.gpsimd.tensor_scalar(out=dst, in0=src, scalar1=1.0, scalar2=0.0, op0=ALU.mult, op1=ALU.add)

        def regroup3(raw, grp, mul, split, order):
            g, v, s = split
            for e in order:
                if e == "g":
                    regroup("g", raw, grp, mul, 0, g)
                elif e == "v":
                    regroup("v", raw, grp, mul, g, g + v)
                else:
                    regroup("s", raw, grp, mul, g + v, g + v + s)

        def quantise(grp, cod, sca):
            nc.vector.quantize_mx(out=cod.bitcast(FP8X4), scales=sca, in_=grp)

        def mx_pass(bank, i, cod, sca):
            nc.tensor.matmul_mx(
                out=bank[:],
                lhsT=zq[:, P * i : P * (i + 1)].bitcast(FP8X4),
                lhsT_scale=zs[:, P * i : P * (i + 1)],
                rhs=cod.bitcast(FP8X4),
                rhs_scale=sca,
                start=True,
                stop=True,
            )

        raw_a = {}
        grp_a = {}
        cod_a = {}
        sca_a = {}

        def load_a(k, parts=((0, 8),)):
            if k not in raw_a:
                raw_a[k] = raw_pool.tile([P, 8, 512], BF16, name="rawt")
            for lo, hi in parts:
                nc.sync.dma_start(
                    out=raw_a[k][:, lo:hi, :], in_=w0[8 * k + lo : 8 * k + hi].rearrange("u (p j) c -> p u (j c)", j=4)
                )

        def load_b(a, lo=0, hi=None):
            w = w2 if a == 0 else w1[16 * (a - 1) : 16 * a]
            hi = hi or (32 if a == 0 else 16)
            nc.sync.dma_start(out=raw_b[a][:, lo:hi, :], in_=w[lo:hi].rearrange("u (p j) c -> p u (j c)", j=4))

        def regroup_a(s, split, order):
            if s not in grp_a:
                grp_a[s] = grpa_pool.tile([P, HALF], BF16, name="grpat", align_bytes=64)
            regroup3(raw_a[s // 2][:, 4 * (s % 2) : 4 * (s % 2) + 4, :], grp_a[s][:], 128, split, order)

        def quantise_a(s):
            cod_a[s] = coda_pool.tile([P, BANK], U32, name="codat", align_bytes=64)
            sca_a[s] = coda_pool.tile([P, BANK], U8, name="scaat", align_bytes=64)
            quantise(grp_a[s][:], cod_a[s][:], sca_a[s][:])

        grp_b = {}

        def regroup_b(m, split, order):
            if m not in grp_b:
                grp_b[m] = grpb_pool.tile([P, 1024], BF16, name="grpbt", align_bytes=64)
            regroup3(raw_b[1 + m // 4][:, 4 * (m % 4) : 4 * (m % 4) + 4, :], grp_b[m][:], 64, split, order)

        def quantise_b(m):
            a, r = 1 + m // 4, m % 4
            quantise(grp_b[m][:], cod_b[a][:, 256 * r : 256 * (r + 1)], sca_b[a][:, 256 * r : 256 * (r + 1)])

        nc.sync.dma_start(out=z_sb[:].rearrange("g (i v) -> g i v", i=TILES), in_=z.rearrange("(i g) v -> g i v", g=P))
        load_a(0, ((0, 4),))
        load_b(0, 0, 8)
        load_b(0, 8, 16)
        nc.sync.dma_start(out=x_sb[:], in_=x.rearrange("(i g) c -> g i c", g=P))
        load_a(0, ((4, 8),))
        load_a(1, ((0, 4), (4, 8)))
        load_a(2)
        load_b(0, 16, 32)

        make_identity(nc, ident[:])
        nc.vector.memset(acc0[:], 0.0)
        fold64 = const.tile([P, 64], F32, name="fold64")
        nc.gpsimd.tensor_tensor(out=fold64[:], in0=ident[:, 0:64], in1=ident[:, 64:128], op=ALU.add)
        fold32 = const.tile([P, 32], F32, name="fold32")
        nc.gpsimd.tensor_tensor(out=fold32[:], in0=fold64[:, 0:32], in1=fold64[:, 32:64], op=ALU.add)
        fold = [fold32, fold64]

        zw = z_sb[:].bitcast(F32).rearrange("g (i p u) -> g i u p", i=TILES, u=2)
        zgf = zg[:].bitcast(F32).rearrange("p (b i g u) -> p b i g u", b=2, i=2, u=2)
        zts = []
        for b in range(2):
            zt = ps_a.tile([P, 2, 2, P], F32, name="bank_a")
            for ii in range(2):
                for u in range(2):
                    nc.tensor.transpose(out=zt[:, ii, u, :], in_=zw[:, 2 * b + ii, u, :], identity=ident[:])
            zts.append(zt)
        nc.vector.tensor_copy(out=zgf[:, 0], in_=zts[0][:].rearrange("p i u g -> p i g u"))
        nc.scalar.copy(out=zgf[:, 1], in_=zts[1][:].rearrange("p i u g -> p i g u"))
        regroup_a(0, SPLIT_P, "vs")
        quantise(zg[:], zq[:], zs[:])
        for b in range(2):
            nc.gpsimd.tensor_scalar(
                out=xs[:, 2 * b : 2 * b + 2, 0:128], in0=x_sb[:, 2 * b : 2 * b + 2, 0:128], scalar1=1.0 / 256.0, scalar2=0.0, op0=ALU.mult, op1=ALU.add
            )
        quantise_a(0)
        grp2 = {}
        grp2[0] = grpb_pool.tile([P, HALF], BF16, name="grp2t", align_bytes=64)
        for b in range(2):
            regroup3(raw_b[0][:, 8 * b : 8 * b + 8, :], grp2[0][:, 1024 * b : 1024 * (b + 1)], 32, SPLIT_P2, "vs")
        nc.scalar.activation(out=xs[:, :, 320:480], in_=x_sb[:, :, 320:480], func=ACT.Copy, scale=1.0 / 128.0)
        nc.vector.quantize_mx(out=cod_b[0][:, 0:BANK].bitcast(FP8X4), scales=sca_b[0][:, 0:BANK], in_=grp2[0][:])
        nc.gpsimd.tensor_scalar(
            out=xs[:, :, 128:320], in0=x_sb[:, :, 128:320], scalar1=1.0 / (64.0 * 512.0) ** 0.5, scalar2=0.0, op0=ALU.mult, op1=ALU.add
        )

        b_banks = [(a, h, i) for a in range(5) for h in range(2) for i in range(TILES)]
        units = []
        for n in range(len(b_banks)):
            for part in range(4 if b_banks[n][0] == 0 else 2):
                units.append((n, part))
        bank_b = {}
        prod = {}
        acc_t = {}

        def b_pass(n):
            a, h, i = b_banks[n]
            bank_b[n] = ps_b.tile([P, BANK], F32, name="bank_b")
            mx_pass(bank_b[n], i, cod_b[a][:, BANK * h : BANK * (h + 1)], sca_b[a][:, BANK * h : BANK * (h + 1)])

        def unit_products(j):
            n, part = units[j]
            a, h, i = b_banks[n]
            prod[j] = prod_pool.tile([P, 768], F32, name="prodt")
            for q in range(4):
                ul = 4 * part + q
                if a == 0:
                    u = 16 * h + ul
                    for m in range(5):
                        slot = 4 * q + m if m < 4 else 16 + q
                        nc.scalar.activation(
                            out=prod[j][:, 32 * slot : 32 * slot + 32],
                            in_=bank_b[n][:, 32 * ul : 32 * ul + 32],
                            func=ACT.Copy,
                            scale=xs[:, i, 320 + 5 * u + m : 320 + 5 * u + m + 1],
                        )
                else:
                    u = 16 * (a - 1) + 8 * h + ul
                    for m in range(3):
                        slot = 6 * (q // 2) + (2 * (q % 2) + m if m < 2 else 4 + q % 2)
                        nc.scalar.activation(
                            out=prod[j][:, 64 * slot : 64 * slot + 64],
                            in_=bank_b[n][:, 64 * ul : 64 * ul + 64],
                            func=ACT.Copy,
                            scale=xs[:, i, 128 + 3 * u + m : 128 + 3 * u + m + 1],
                        )

        first_sum = {}

        def unit_sums(j):
            n, part = units[j]
            a, h, i = b_banks[n]
            blk = 0 if a == 0 else 1
            if blk not in acc_t:
                acc_t[blk] = (ps_acc.tile([P, N], F32, name="acc_x"), ps_acc.tile([P, N], F32, name="acc_y"))
            last_unit = 31 if a == 0 else 95
            kinds = [0, 0, 0, 0, 1] if a == 0 else [0, 0, 1, 0, 0, 1]
            for b in range(len(kinds)):
                kd = kinds[b]
                nc.tensor.matmul(
                    out=acc_t[blk][kd][:, P * i : P * (i + 1)],
                    lhsT=prod[j][:, P * b : P * (b + 1)],
                    rhs=ident[:],
                    is_transpose=True,
                    start=((blk, kd) not in first_sum),
                    stop=(j == last_unit and b == (len(kinds) - 1 if kd == 1 else len(kinds) - 2)),
                )
                first_sum[(blk, kd)] = True

        t_sb = {}

        def evacuate(blk, engines, pieces):
            for kd in range(2):
                t_sb[(blk, kd)] = const.tile([P, N], F32, name="t_sb%d%d" % (blk, kd))
            w = N // pieces
            for g in range(pieces):
                for kd in range(2):
                    if engines[kd] == "s":
                        nc.scalar.copy(out=t_sb[(blk, kd)][:, w * g : w * (g + 1)], in_=acc_t[blk][kd][:, w * g : w * (g + 1)])
                    else:
                        nc.vector.tensor_copy(out=t_sb[(blk, kd)][:, w * g : w * (g + 1)], in_=acc_t[blk][kd][:, w * g : w * (g + 1)])

        def finish(blk, pool, tag, copier):
            mul, d, off = (32, 5, 320) if blk == 0 else (64, 3, 128)
            for b in range(2):
                b_ps = pool.tile([P, 2, d * mul], F32, name=tag)
                for ii in range(2):
                    i = 2 * b + ii
                    nc.tensor.transpose(out=b_ps[:, ii, 0:P], in_=t_sb[(blk, 0)][:, P * i : P * (i + 1)], identity=ident[:])
                    nc.tensor.matmul(
                        out=b_ps[:, ii, P : P + mul],
                        lhsT=t_sb[(blk, 1)][:, P * i : P * (i + 1)],
                        rhs=fold[blk][:],
                        start=True,
                        stop=True,
                    )
                dst = fin[:, 2 * b : 2 * b + 2, off : off + mul * d].rearrange("p i (c m) -> p i c m", m=d)
                if copier[b] == "s":
                    nc.scalar.copy(out=dst, in_=b_ps[:].rearrange("p i (m c) -> p i c m", c=mul))
                else:
                    nc.vector.tensor_copy(out=dst, in_=b_ps[:].rearrange("p i (m c) -> p i c m", c=mul))
                nc.sync.dma_start(out=out_v[:, 2 * b : 2 * b + 2, off : off + mul * d], in_=fin[:, 2 * b : 2 * b + 2, off : off + mul * d])

        state = {"bank": 2, "deferred": False}

        def unit_lo(t):
            return min(96, (U_NUM * t) // U_DEN)

        b_step = {}
        for m in range(16):
            b_step[B_OFF + (B_NUM * m) // B_DEN] = m
        out_v = out.rearrange("(i g) c -> g i c", g=P)
        bank_a = {}

        def port_work(t):
            if t == 3:
                nc.vector.quantize_mx(out=cod_b[0][:, BANK : 2 * BANK].bitcast(FP8X4), scales=sca_b[0][:, BANK : 2 * BANK], in_=grp2[1][:])
            if t + 1 < STEPS:
                quantise_a(t + 1)
            if (t - 1) in b_step:
                quantise_b(b_step[t - 1])
            if t == 0:
                regroup_a(2, SPLIT_P, "v")
            if t == 2:
                grp2[1] = grpb_pool.tile([P, HALF], BF16, name="grp2t", align_bytes=64)
                regroup3(raw_b[0][:, 16:32, :], grp2[1][:], 32, SPLIT_P2, "v")
            for e in "vg":
                if t in b_step:
                    regroup_b(b_step[t], SPLIT_B, e)
                if t + 3 < STEPS:
                    regroup_a(t + 3, SPLIT_3 if t == 0 else SPLIT_A, e)

        def macs(t, pair):
            for q in range(4):
                for i in (2 * pair, 2 * pair + 1):
                    u = 4 * t + q
                    nc.vector.scalar_tensor_tensor(
                        out=acc0[:, q % 2, i, :],
                        in0=bank_a[i][:, P * q : P * (q + 1)],
                        scalar=xs[:, i, u : u + 1],
                        in1=acc0[:, q % 2, i, :],
                        op0=ALU.mult,
                        op1=ALU.add,
                    )

        def unit(j, t):
            n, part = units[j]
            if part == 0 and j > 0 and state["bank"] < len(b_banks):
                per_bank = 4 if b_banks[n][0] == 0 else 2
                if j > unit_lo(t) and j + per_bank > unit_lo(t + 1):
                    state["deferred"] = True
                else:
                    b_pass(state["bank"])
                    state["bank"] = state["bank"] + 1
            if j == 33:
                evacuate(0, "ss", 1)
            if j - LAG >= 0:
                unit_sums(j - LAG)
            unit_products(j)
            if j == 0:
                regroup_a(1, SPLIT_P, "s")
                regroup_a(2, SPLIT_P, "s")
            if j == max(unit_lo(t), 1):
                if t == 2:
                    regroup3(raw_b[0][:, 16:32, :], grp2[1][:], 32, SPLIT_P2, "s")
                if t + 3 < STEPS:
                    regroup_a(t + 3, SPLIT_3 if t == 0 else SPLIT_A, "s")
                if t in b_step:
                    regroup_b(b_step[t], SPLIT_B, "s")

        for t in range(STEPS):
            if t == 0:
                load_a(3)
                load_b(1)
            if t % 2 == 0 and t // 2 + 4 < 16:
                load_a(t // 2 + 4)
            if t in (4, 10, 16):
                load_b(2 + (t - 4) // 6)
            if t > 0:
                port_work(t)
            if state["deferred"]:
                b_pass(state["bank"])
                state["bank"] = state["bank"] + 1
                state["deferred"] = False
            for i in range(TILES):
                bank_a[i] = ps_a.tile([P, BANK], F32, name="bank_a")
                mx_pass(bank_a[i], i, cod_a[t][:], sca_a[t][:])
                if t == 0 and i % 2 == 1:
                    b_pass(i // 2)
            macs(t, 0)
            if t == 0:
                regroup_a(1, SPLIT_P, "v")
                unit(0, 0)
                port_work(0)
            macs(t, 1)
            for j in range(max(unit_lo(t), 1), unit_lo(t + 1)):
                unit(j, t)
        for j in range(96 - LAG, 96):
            unit_sums(j)

        nc.vector.tensor_tensor(out=fin[:, :, 0:128], in0=acc0[:, 0], in1=acc0[:, 1], op=ALU.add)
        nc.sync.dma_start(out=out_v[:, :, 0:128], in_=fin[:, :, 0:128])
        evacuate(1, "sv", 2)
        finish(0, ps_a, "bank_a", "sv")
        finish(1, ps_b, "bank_b", "sv")
